import numpy as np
import ml_dtypes


def mxq(x, axis, fmt="e4m3"):
    dtype, down = {"e4m3": (ml_dtypes.float8_e4m3fn, 7), "e5m2": (ml_dtypes.float8_e5m2, 14)}[fmt]
    v = np.moveaxis(np.asarray(x, np.float32).astype(ml_dtypes.bfloat16).astype(np.float64), axis, -1)
    blocks = v.reshape(v.shape[:-1] + (-1, 32))
    amax = np.abs(blocks).max(-1, keepdims=True)
    byte = np.maximum(np.where(amax > 0, np.frexp(amax)[1] - 1 + 127, 0) - down, 1)
    scale = np.exp2(byte - 127.0)
    codes = (blocks / scale).astype(np.float32).astype(dtype).astype(np.float64)
    return np.moveaxis((codes * scale).reshape(v.shape), -1, axis)


WIDE = False


def mx_kscale(k):
    if not WIDE:
        return np.ones(k)
    levels = np.array([20, -20, 10, -10, 0])
    if k % 512:
        return np.exp2(np.random.permutation(np.resize(levels, k // 32))).repeat(32)
    a = np.empty((k // 512, 16))
    for p in range(k // 512):
        a[p, :8] = np.random.permutation(np.resize(levels, 8))
        for g in range(8):
            far = levels[np.abs(levels - a[p, g]) >= 10]
            a[p, g + 8] = far[np.random.randint(len(far))]
    return np.exp2(a.ravel()).repeat(32)


BF16 = ml_dtypes.bfloat16


def bf(x):
    return np.asarray(x, np.float32).astype(BF16)


def f64(x):
    return np.asarray(x).astype(np.float64)


B, S, D_IN, D_OUT = 3, 512, 256, 8192


def relative_shift(x):
    b, s, d = x.shape
    padded = np.concatenate([np.zeros((b, 1, d)), x], axis=1).reshape(s + 1, b, d)
    return padded[1:].reshape(b, s, d)


def relative_shift_adjoint(g, b, s):
    d = g.shape[1]
    padded = np.concatenate([np.zeros((b, d)), g], axis=0).reshape(b, s + 1, d)
    return padded[:, 1:]


def setup_inputs():
    u = mx_kscale(D_OUT)
    pos_embed = np.random.standard_normal((B, S, D_IN))
    W_r = np.random.standard_normal((D_OUT, D_IN)) * 1.2 / np.sqrt(D_IN) / u[:, None]
    b_r = np.random.standard_normal(D_OUT) * 0.3
    g = np.random.standard_normal((B, S, D_OUT)) * np.exp2(np.random.randint(-12, 1, (B, S, 1))) * 8.0 * u
    return {"pos_embed": bf(pos_embed), "W_r": bf(W_r), "b_r": bf(b_r), "grad_out": bf(g)}


def reference(pos_embed, W_r, b_r, grad_out):
    g = f64(grad_out).reshape(B * S, D_OUT)
    gs = mxq(g, 1, "e5m2") @ mxq(f64(W_r), 0, "e4m3")
    return relative_shift_adjoint(gs, B, S)

@@ -1,0 +1,222 @@
+from contextlib import ExitStack
+
+import concourse.mybir as mybir
+from concourse.masks import make_identity
+
+F32 = mybir.dt.float32
+BF16 = mybir.dt.bfloat16
+U32 = mybir.dt.uint32
+U8 = mybir.dt.uint8
+E4M3X4 = mybir.dt.float8_e4m3fn_x4
+E5M2X4 = mybir.dt.float8_e5m2_x4
+
+BATCH, SEQ, D_IN, D_OUT = 3, 512, 256, 8192
+TOKENS = BATCH * SEQ
+
+P = 128
+PACK = 4
+K_PASS = P * PACK
+PASSES = D_OUT // K_PASS
+GROUP = 512
+GROUPS = TOKENS // GROUP
+SUBTILES = GROUP // P
+M_TILES = D_IN // P
+HALF_WORDS = K_PASS // 4
+
+LOAD_PASSES = 4
+LOAD_K = LOAD_PASSES * K_PASS
+LOADS = PASSES // LOAD_PASSES
+RUN_PASSES = 4
+GRAD_BUFS = 5
+
+FLOPS = 2 * TOKENS * D_OUT * D_IN
+BYTES = 2 * TOKENS * D_OUT + 2 * D_OUT * D_IN + 4 * TOKENS * D_IN
+
+
+def tile_relativemultiheadattention_pa_k_kernel(tc, pos_embed, W_r, b_r, grad_out, out):
+    nc = tc.nc
+    grad_rows = grad_out.flatten_outer_dims()
+    out_rows = out.flatten_outer_dims()
+
+    with ExitStack() as ctx:
+        keep = ctx.enter_context(tc.tile_pool(name="keep", bufs=1))
+        grad_pool = ctx.enter_context(tc.tile_pool(name="grad", bufs=GRAD_BUFS))
+        w_raw_pool = ctx.enter_context(tc.tile_pool(name="w_raw", bufs=LOADS))
+        w_grouped_pool = ctx.enter_context(tc.tile_pool(name="w_grouped", bufs=2))
+        grouped_pool = ctx.enter_context(tc.tile_pool(name="grouped", bufs=RUN_PASSES + 2))
+        operand_pool = ctx.enter_context(tc.tile_pool(name="operand", bufs=2 * RUN_PASSES + 1))
+        result_pool = ctx.enter_context(tc.tile_pool(name="result", bufs=4))
+        acc_pool = ctx.enter_context(tc.psum_pool(name="acc", bufs=1))
+        bank_pool = ctx.enter_context(tc.psum_pool(name="bank", bufs=8 - M_TILES))
+        ctx.enter_context(tc.manual_schedule())
+
+        identity = keep.tile([P, P], F32, name="identity")
+        make_identity(nc, identity[:])
+
+        w_codes = keep.tile([P, PASSES, D_IN], U32, name="w_codes", align_bytes=64)
+        w_scales = keep.tile([P, PASSES, D_IN], U8, name="w_scales", align_bytes=64)
+
+        g_t = [keep.tile([P, TOKENS], F32, name="g_t%d" % m) for m in range(M_TILES)]
+        for m in range(M_TILES):
+            nc.vector.memset(g_t[m][:, 0:8], 0.0)
+
+        def load_grad(index):
+            n, q = divmod(index, LOADS)
+            raw = grad_pool.tile([P, SUBTILES, LOAD_K], BF16, name="grad_raw")
+            rows = grad_rows[n * GROUP : (n + 1) * GROUP, q * LOAD_K : (q + 1) * LOAD_K]
+            nc.sync.dma_start(out=raw[:], in_=rows.rearrange("(s p) k -> p s k", p=P))
+            return raw
+
+        def load_weights(q):
+            raw = w_raw_pool.tile([P, LOAD_PASSES, PACK, D_IN], BF16, name="w_raw")
+            rows = W_r[q * LOAD_K : (q + 1) * LOAD_K, :]
+            nc.sync.dma_start(
+                out=raw[:].rearrange("p g t d -> p g (t d)"),
+                in_=rows.rearrange("(g p t) d -> p g (t d)", p=P, t=PACK),
+            )
+            return raw
+
+        def regroup_weights(raw, first_pass):
+            grouped = w_grouped_pool.tile([P, RUN_PASSES, D_IN, PACK], BF16, name="w_grouped", align_bytes=64)
+            for j in range(RUN_PASSES):
+                nc.vector.tensor_copy(
+                    out=grouped[:, j, :, :].rearrange("p (c i) t -> p c t i", i=4),
+                    in_=raw[:, first_pass % LOAD_PASSES + j, :, :].rearrange("p t (c i) -> p c t i", i=4),
+                )
+            return grouped
+
+        def quantise_weights(grouped, first_pass):
+            passes = slice(first_pass, first_pass + RUN_PASSES)
+            nc.vector.quantize_mx(
+                out=w_codes[:, passes, :].rearrange("p c d -> p (c d)").bitcast(E4M3X4),
+                scales=w_scales[:, passes, :].rearrange("p c d -> p (c d)"),
+                in_=grouped[:].rearrange("p c d t -> p (c d t)"),
+            )
+
+        def transpose_run(raw, n, first_pass):
+            operands = []
+            grouped_tiles = []
+
+            def quantise_pass(j):
+                codes = operand_pool.tile([P, GROUP], U32, name="grad_codes", align_bytes=64)
+                scales = operand_pool.tile([P, GROUP], U8, name="grad_scales", align_bytes=64)
+                nc.vector.quantize_mx(
+                    out=codes[:].bitcast(E5M2X4),
+                    scales=scales[:],
+                    in_=grouped_tiles[j][:].rearrange("p r t -> p (r t)"),
+                )
+                operands.append((first_pass + j, codes, scales))
+
+            for j in range(RUN_PASSES):
+                word0 = ((first_pass + j) % LOAD_PASSES) * 2 * HALF_WORDS
+                grouped = grouped_pool.tile([P, GROUP, PACK], BF16, name="grouped", align_bytes=64)
+                grouped_tiles.append(grouped)
+                for half in range(2):
+                    bank = bank_pool.tile([P, 2, 2 * P], F32, name="bank")
+                    for u in range(2):
+                        for s in range(2):
+                            words = raw[:, 2 * half + s, :].bitcast(F32)
+                            nc.tensor.transpose(
+                                bank[:, u, s * P : (s + 1) * P],
+                                words[:, word0 + u : word0 + 2 * HALF_WORDS : 2],
+                                identity[:],
+                            )
+                    tokens = slice(half * 2 * P, (half + 1) * 2 * P)
+                    pairs = (
+                        grouped[:, tokens, :]
+                        .rearrange("p r t -> p (r t)")
+                        .bitcast(F32)
+                        .rearrange("p (r u) -> p r u", u=2)
+                    )
+                    if n > 0 and j % 2 == 1 and half == 1:
+                        nc.vector.tensor_copy(out=pairs, in_=bank[:].rearrange("p u r -> p r u"))
+                    else:
+                        nc.scalar.copy(out=pairs, in_=bank[:].rearrange("p u r -> p r u"))
+                if j > 0:
+                    quantise_pass(j - 1)
+            quantise_pass(RUN_PASSES - 1)
+            return operands
+
+        def multiply_run(operands, acc):
+            for c, codes, scales in operands:
+                for m in range(M_TILES):
+                    columns = slice(m * P, (m + 1) * P)
+                    nc.tensor.matmul_mx(
+                        out=acc[m][:],
+                        lhsT=w_codes[:, c, columns].bitcast(E4M3X4),
+                        lhsT_scale=w_scales[:, c, columns],
+                        rhs=codes[:].bitcast(E5M2X4),
+                        rhs_scale=scales[:],
+                        start=(c == 0),
+                        stop=(c == PASSES - 1),
+                    )
+
+        def shift_out_of_psum(n, acc):
+            for m in range(M_TILES):
+                for b in range(BATCH):
+                    first_s = max(0, 2 - (SEQ + 1) * b)
+                    lo = max((SEQ + 1) * b + first_s - 2, n * GROUP)
+                    hi = min((SEQ + 1) * b + SEQ - 2, (n + 1) * GROUP)
+                    if lo < hi:
+                        src = acc[m][:, lo - n * GROUP : hi - n * GROUP]
+                        dst = g_t[m][:, lo + 2 - b : hi + 2 - b]
+                        if m == 0:
+                            nc.scalar.copy(out=dst, in_=src)
+                        else:
+                            nc.vector.tensor_copy(out=dst, in_=src)
+
+        def store_group(n):
+            for pair in range(SUBTILES // 2):
+                row0 = n * GROUP + pair * 2 * P
+                bank = bank_pool.tile([P, 2, D_IN], F32, name="bank")
+                for j in range(2):
+                    for m in range(M_TILES):
+                        nc.tensor.transpose(
+                            bank[:, j, m * P : (m + 1) * P],
+                            g_t[m][:, row0 + j * P : row0 + (j + 1) * P],
+                            identity[:],
+                        )
+                result = result_pool.tile([P, 2, D_IN], F32, name="result")
+                if pair == 0:
+                    nc.scalar.copy(out=result[:], in_=bank[:])
+                else:
+                    nc.vector.tensor_copy(out=result[:], in_=bank[:])
+                nc.sync.dma_start(
+                    out=out_rows[row0 : row0 + 2 * P, :].rearrange("(j p) d -> p j d", p=P),
+                    in_=result[:],
+                )
+
+        grad_tiles = {}
+        w_tiles = {}
+        for index in range(GRAD_BUFS):
+            grad_tiles[index] = load_grad(index)
+            if index < LOADS:
+                w_tiles[index] = load_weights(index)
+
+        acc = None
+        waiting = None
+        to_store = None
+        for n in range(GROUPS):
+            for first_pass in range(0, PASSES, RUN_PASSES):
+                index = n * LOADS + first_pass // LOAD_PASSES
+                if n == 0:
+                    w_grouped = regroup_weights(w_tiles[index], first_pass)
+                operands = transpose_run(grad_tiles[index], n, first_pass)
+                if n == 0:
+                    quantise_weights(w_grouped, first_pass)
+                if (first_pass + RUN_PASSES) % LOAD_PASSES == 0 and index + GRAD_BUFS < GROUPS * LOADS:
+                    grad_tiles[index + GRAD_BUFS] = load_grad(index + GRAD_BUFS)
+                if to_store is not None:
+                    store_group(to_store)
+                    to_store = None
+                if waiting is not None:
+                    multiply_run(waiting, acc)
+                    if first_pass == 0:
+                        shift_out_of_psum(n - 1, acc)
+                        to_store = n - 1
+                if first_pass == 0:
+                    acc = [acc_pool.tile([P, GROUP], F32, name="acc%d" % m) for m in range(M_TILES)]
+                waiting = operands
+        multiply_run(waiting, acc)
+        shift_out_of_psum(GROUPS - 1, acc)
+        store_group(GROUPS - 1)

@@ -16,18 +16,19 @@ TOKENS = BATCH * SEQ
 P = 128
 PACK = 4
 K_PASS = P * PACK
+WORDS = K_PASS // 2
 PASSES = D_OUT // K_PASS
 GROUP = 512
 GROUPS = TOKENS // GROUP
-SUBTILES = GROUP // P
 M_TILES = D_IN // P
-HALF_WORDS = K_PASS // 4
 
 LOAD_PASSES = 4
 LOAD_K = LOAD_PASSES * K_PASS
-LOADS = PASSES // LOAD_PASSES
-RUN_PASSES = 4
-GRAD_BUFS = 5
+CHUNKS = PASSES // LOAD_PASSES
+PAIR = 2
+PAIRS = GROUP // (PAIR * P)
+SORTED = 6
+RUN_PASSES = 2
 
 FLOPS = 2 * TOKENS * D_OUT * D_IN
 BYTES = 2 * TOKENS * D_OUT + 2 * D_OUT * D_IN + 4 * TOKENS * D_IN
@@ -40,14 +41,14 @@ def tile_relativemultiheadattention_pa_k_kernel(tc, pos_embed, W_r, b_r, grad_ou
 
     with ExitStack() as ctx:
         keep = ctx.enter_context(tc.tile_pool(name="keep", bufs=1))
-        grad_pool = ctx.enter_context(tc.tile_pool(name="grad", bufs=GRAD_BUFS))
-        w_raw_pool = ctx.enter_context(tc.tile_pool(name="w_raw", bufs=LOADS))
+        grad_pool = ctx.enter_context(tc.tile_pool(name="grad", bufs=8))
+        w_raw_pool = ctx.enter_context(tc.tile_pool(name="w_raw", bufs=3))
         w_grouped_pool = ctx.enter_context(tc.tile_pool(name="w_grouped", bufs=2))
-        grouped_pool = ctx.enter_context(tc.tile_pool(name="grouped", bufs=RUN_PASSES + 2))
-        operand_pool = ctx.enter_context(tc.tile_pool(name="operand", bufs=2 * RUN_PASSES + 1))
+        ordered_pool = ctx.enter_context(tc.tile_pool(name="ordered", bufs=5))
+        grouped_pool = ctx.enter_context(tc.tile_pool(name="grouped", bufs=6))
+        operand_pool = ctx.enter_context(tc.tile_pool(name="operand", bufs=10))
         result_pool = ctx.enter_context(tc.tile_pool(name="result", bufs=4))
-        acc_pool = ctx.enter_context(tc.psum_pool(name="acc", bufs=1))
-        bank_pool = ctx.enter_context(tc.psum_pool(name="bank", bufs=8 - M_TILES))
+        psum = ctx.enter_context(tc.psum_pool(name="psum", bufs=1))
         ctx.enter_context(tc.manual_schedule())
 
         identity = keep.tile([P, P], F32, name="identity")
@@ -60,103 +61,116 @@ def tile_relativemultiheadattention_pa_k_kernel(tc, pos_embed, W_r, b_r, grad_ou
         for m in range(M_TILES):
             nc.vector.memset(g_t[m][:, 0:8], 0.0)
 
-        def load_grad(index):
-            n, q = divmod(index, LOADS)
-            raw = grad_pool.tile([P, SUBTILES, LOAD_K], BF16, name="grad_raw")
-            rows = grad_rows[n * GROUP : (n + 1) * GROUP, q * LOAD_K : (q + 1) * LOAD_K]
-            nc.sync.dma_start(out=raw[:], in_=rows.rearrange("(s p) k -> p s k", p=P))
-            return raw
+        raws, w_raws = {}, {}
 
-        def load_weights(q):
+        def load_grad(n, pair, chunk):
+            raw = grad_pool.tile([P, PAIR, LOAD_PASSES, K_PASS], BF16, name="grad_raw")
+            row0 = n * GROUP + pair * PAIR * P
+            rows = grad_rows[row0 : row0 + PAIR * P, chunk * LOAD_K : (chunk + 1) * LOAD_K]
+            nc.sync.dma_start(
+                out=raw[:].rearrange("p s g k -> p s (g k)"),
+                in_=rows.rearrange("(s p) k -> p s k", p=P),
+            )
+            raws[(n, pair, chunk)] = raw
+
+        def load_weights(chunk):
             raw = w_raw_pool.tile([P, LOAD_PASSES, PACK, D_IN], BF16, name="w_raw")
-            rows = W_r[q * LOAD_K : (q + 1) * LOAD_K, :]
+            rows = W_r[chunk * LOAD_K : (chunk + 1) * LOAD_K, :]
             nc.sync.dma_start(
                 out=raw[:].rearrange("p g t d -> p g (t d)"),
                 in_=rows.rearrange("(g p t) d -> p g (t d)", p=P, t=PACK),
             )
-            return raw
+            w_raws[chunk] = raw
 
-        def regroup_weights(raw, first_pass):
-            grouped = w_grouped_pool.tile([P, RUN_PASSES, D_IN, PACK], BF16, name="w_grouped", align_bytes=64)
-            for j in range(RUN_PASSES):
+        def prepare_weights(chunk, passes):
+            raw = w_raws[chunk]
+            grouped = w_grouped_pool.tile([P, LOAD_PASSES, D_IN, PACK], BF16, name="w_grouped", align_bytes=64)
+            for j in range(LOAD_PASSES):
                 nc.vector.tensor_copy(
                     out=grouped[:, j, :, :].rearrange("p (c i) t -> p c t i", i=4),
-                    in_=raw[:, first_pass % LOAD_PASSES + j, :, :].rearrange("p t (c i) -> p c t i", i=4),
+                    in_=raw[:, j, :, :].rearrange("p t (c i) -> p c t i", i=4),
                 )
             return grouped
 
-        def quantise_weights(grouped, first_pass):
-            passes = slice(first_pass, first_pass + RUN_PASSES)
+        def quantise_weights(grouped, chunk):
+            passes = slice(chunk * LOAD_PASSES, (chunk + 1) * LOAD_PASSES)
             nc.vector.quantize_mx(
                 out=w_codes[:, passes, :].rearrange("p c d -> p (c d)").bitcast(E4M3X4),
                 scales=w_scales[:, passes, :].rearrange("p c d -> p (c d)"),
                 in_=grouped[:].rearrange("p c d t -> p (c d t)"),
             )
 
-        def transpose_run(raw, n, first_pass):
-            operands = []
-            grouped_tiles = []
+        ordered = {}
 
-            def quantise_pass(j):
-                codes = operand_pool.tile([P, GROUP], U32, name="grad_codes", align_bytes=64)
-                scales = operand_pool.tile([P, GROUP], U8, name="grad_scales", align_bytes=64)
-                nc.vector.quantize_mx(
-                    out=codes[:].bitcast(E5M2X4),
-                    scales=scales[:],
-                    in_=grouped_tiles[j][:].rearrange("p r t -> p (r t)"),
+        def sort_words(key):
+            if SORTED > 0:
+                tile = ordered_pool.tile([P, SORTED, 2, P], F32, name="ordered")
+                rows = raws[key][:].rearrange("p s g k -> p (s g) k")[:, 0:SORTED, :]
+                nc.vector.tensor_copy(
+                    out=tile[:],
+                    in_=rows.bitcast(F32).rearrange("p x (j u) -> p x u j", u=2),
                 )
-                operands.append((first_pass + j, codes, scales))
+                ordered[key] = tile
 
-            for j in range(RUN_PASSES):
-                word0 = ((first_pass + j) % LOAD_PASSES) * 2 * HALF_WORDS
-                grouped = grouped_pool.tile([P, GROUP, PACK], BF16, name="grouped", align_bytes=64)
-                grouped_tiles.append(grouped)
-                for half in range(2):
-                    bank = bank_pool.tile([P, 2, 2 * P], F32, name="bank")
+        def words_of(key, s, c, u):
+            x = s * LOAD_PASSES + c
+            if x < SORTED:
+                return ordered[key][:, x, u, :]
+            return raws[key][:, s, c, :].bitcast(F32)[:, u:WORDS:2]
+
+        bank_turn = [0]
+
+        def transpose_pass(n, c, banks):
+            grouped = grouped_pool.tile([P, GROUP, PACK], BF16, name="grouped", align_bytes=64)
+            chunk, c_in = divmod(c, LOAD_PASSES)
+            for pair in range(PAIRS):
+                bank = psum.tile([P, 2, PAIR * P], F32, name="bank%d" % banks[bank_turn[0] % len(banks)])
+                bank_turn[0] += 1
+                for s in range(PAIR):
                     for u in range(2):
-                        for s in range(2):
-                            words = raw[:, 2 * half + s, :].bitcast(F32)
-                            nc.tensor.transpose(
-                                bank[:, u, s * P : (s + 1) * P],
-                                words[:, word0 + u : word0 + 2 * HALF_WORDS : 2],
-                                identity[:],
-                            )
-                    tokens = slice(half * 2 * P, (half + 1) * 2 * P)
-                    pairs = (
-                        grouped[:, tokens, :]
-                        .rearrange("p r t -> p (r t)")
-                        .bitcast(F32)
-                        .rearrange("p (r u) -> p r u", u=2)
-                    )
-                    if n > 0 and j % 2 == 1 and half == 1:
-                        nc.vector.tensor_copy(out=pairs, in_=bank[:].rearrange("p u r -> p r u"))
-                    else:
-                        nc.scalar.copy(out=pairs, in_=bank[:].rearrange("p u r -> p r u"))
-                if j > 0:
-                    quantise_pass(j - 1)
-            quantise_pass(RUN_PASSES - 1)
-            return operands
+                        nc.tensor.transpose(
+                            bank[:, u, s * P : (s + 1) * P],
+                            words_of((n, pair, chunk), s, c_in, u),
+                            identity[:],
+                        )
+                words = (
+                    grouped[:, pair * PAIR * P : (pair + 1) * PAIR * P, :]
+                    .rearrange("p r t -> p (r t)")
+                    .bitcast(F32)
+                    .rearrange("p (r u) -> p r u", u=2)
+                )
+                nc.scalar.copy(out=words, in_=bank[:].rearrange("p u r -> p r u"))
+            return grouped
 
-        def multiply_run(operands, acc):
-            for c, codes, scales in operands:
-                for m in range(M_TILES):
-                    columns = slice(m * P, (m + 1) * P)
-                    nc.tensor.matmul_mx(
-                        out=acc[m][:],
-                        lhsT=w_codes[:, c, columns].bitcast(E4M3X4),
-                        lhsT_scale=w_scales[:, c, columns],
-                        rhs=codes[:].bitcast(E5M2X4),
-                        rhs_scale=scales[:],
-                        start=(c == 0),
-                        stop=(c == PASSES - 1),
-                    )
+        def quantise_pass(grouped):
+            codes = operand_pool.tile([P, GROUP], U32, name="grad_codes", align_bytes=64)
+            scales = operand_pool.tile([P, GROUP], U8, name="grad_scales", align_bytes=64)
+            nc.vector.quantize_mx(
+                out=codes[:].bitcast(E5M2X4),
+                scales=scales[:],
+                in_=grouped[:].rearrange("p r t -> p (r t)"),
+            )
+            return codes, scales
 
-        def shift_out_of_psum(n, acc):
+        def multiply_pass(operand, c, acc):
+            codes, scales = operand
+            for m in range(M_TILES):
+                columns = slice(m * P, (m + 1) * P)
+                nc.tensor.matmul_mx(
+                    out=acc[m][:],
+                    lhsT=w_codes[:, c, columns].bitcast(E4M3X4),
+                    lhsT_scale=w_scales[:, c, columns],
+                    rhs=codes[:].bitcast(E5M2X4),
+                    rhs_scale=scales[:],
+                    start=(c == 0),
+                    stop=(c == PASSES - 1),
+                )
+
+        def shift_out_of_psum(n, acc, first, last):
             for m in range(M_TILES):
                 for b in range(BATCH):
-                    first_s = max(0, 2 - (SEQ + 1) * b)
-                    lo = max((SEQ + 1) * b + first_s - 2, n * GROUP)
-                    hi = min((SEQ + 1) * b + SEQ - 2, (n + 1) * GROUP)
+                    lo = max((SEQ + 1) * b - 2, n * GROUP + first)
+                    hi = min((SEQ + 1) * b - 2 + SEQ, n * GROUP + last)
                     if lo < hi:
                         src = acc[m][:, lo - n * GROUP : hi - n * GROUP]
                         dst = g_t[m][:, lo + 2 - b : hi + 2 - b]
@@ -165,58 +179,104 @@ def tile_relativemultiheadattention_pa_k_kernel(tc, pos_embed, W_r, b_r, grad_ou
                         else:
                             nc.vector.tensor_copy(out=dst, in_=src)
 
-        def store_group(n):
-            for pair in range(SUBTILES // 2):
-                row0 = n * GROUP + pair * 2 * P
-                bank = bank_pool.tile([P, 2, D_IN], F32, name="bank")
-                for j in range(2):
-                    for m in range(M_TILES):
-                        nc.tensor.transpose(
-                            bank[:, j, m * P : (m + 1) * P],
-                            g_t[m][:, row0 + j * P : row0 + (j + 1) * P],
-                            identity[:],
-                        )
-                result = result_pool.tile([P, 2, D_IN], F32, name="result")
-                if pair == 0:
-                    nc.scalar.copy(out=result[:], in_=bank[:])
+        def transpose_back(n, pair, banks):
+            row0 = n * GROUP + pair * 2 * P
+            bank = psum.tile([P, 2, D_IN], F32, name="bank%d" % banks[bank_turn[0] % len(banks)])
+            bank_turn[0] += 1
+            for j in range(2):
+                for m in range(M_TILES):
+                    nc.tensor.transpose(
+                        bank[:, j, m * P : (m + 1) * P],
+                        g_t[m][:, row0 + j * P : row0 + (j + 1) * P],
+                        identity[:],
+                    )
+            result = result_pool.tile([P, 2, D_IN], F32, name="result")
+            if pair == 0:
+                nc.scalar.copy(out=result[:], in_=bank[:])
+            else:
+                nc.vector.tensor_copy(out=result[:], in_=bank[:])
+            nc.sync.dma_start(
+                out=out_rows[row0 : row0 + 2 * P, :].rearrange("(j p) d -> p j d", p=P),
+                in_=result[:],
+            )
+
+        HEAD_GROUPS = 2
+        loads = []
+        steps = []
+        for chunk in range(CHUNKS):
+            for n in range(HEAD_GROUPS):
+                loads += [(n, pair, chunk) for pair in range(PAIRS)]
+                if n == 0:
+                    loads.append(chunk)
+            for first in range(0, LOAD_PASSES, RUN_PASSES):
+                for n in range(HEAD_GROUPS):
+                    steps.append((n, chunk * LOAD_PASSES + first))
+        for n in range(HEAD_GROUPS, GROUPS):
+            for chunk in range(CHUNKS):
+                loads += [(n, pair, chunk) for pair in range(PAIRS)]
+                for first in range(0, LOAD_PASSES, RUN_PASSES):
+                    steps.append((n, chunk * LOAD_PASSES + first))
+        acc_banks = {0: (0, 1), 1: (2, 3), 2: (0, 1)}
+
+        AHEAD = 8
+        issued = [0]
+
+        def issue_loads(count):
+            while issued[0] < min(count, len(loads)):
+                item = loads[issued[0]]
+                issued[0] += 1
+                if item in range(CHUNKS):
+                    load_weights(item)
                 else:
-                    nc.vector.tensor_copy(out=result[:], in_=bank[:])
-                nc.sync.dma_start(
-                    out=out_rows[row0 : row0 + 2 * P, :].rearrange("(j p) d -> p j d", p=P),
-                    in_=result[:],
-                )
+                    load_grad(*item)
 
-        grad_tiles = {}
-        w_tiles = {}
-        for index in range(GRAD_BUFS):
-            grad_tiles[index] = load_grad(index)
-            if index < LOADS:
-                w_tiles[index] = load_weights(index)
+        def keys_of(s):
+            n, first = steps[s]
+            return [(n, pair, first // LOAD_PASSES) for pair in range(PAIRS)]
 
-        acc = None
-        waiting = None
-        to_store = None
-        for n in range(GROUPS):
-            for first_pass in range(0, PASSES, RUN_PASSES):
-                index = n * LOADS + first_pass // LOAD_PASSES
-                if n == 0:
-                    w_grouped = regroup_weights(w_tiles[index], first_pass)
-                operands = transpose_run(grad_tiles[index], n, first_pass)
-                if n == 0:
-                    quantise_weights(w_grouped, first_pass)
-                if (first_pass + RUN_PASSES) % LOAD_PASSES == 0 and index + GRAD_BUFS < GROUPS * LOADS:
-                    grad_tiles[index + GRAD_BUFS] = load_grad(index + GRAD_BUFS)
-                if to_store is not None:
-                    store_group(to_store)
-                    to_store = None
-                if waiting is not None:
-                    multiply_run(waiting, acc)
-                    if first_pass == 0:
-                        shift_out_of_psum(n - 1, acc)
-                        to_store = n - 1
-                if first_pass == 0:
-                    acc = [acc_pool.tile([P, GROUP], F32, name="acc%d" % m) for m in range(M_TILES)]
-                waiting = operands
-        multiply_run(waiting, acc)
-        shift_out_of_psum(GROUPS - 1, acc)
-        store_group(GROUPS - 1)
+        def sort_step(s):
+            for key in keys_of(s):
+                if key not in ordered:
+                    sort_words(key)
+
+        issue_loads(AHEAD)
+        grouped, operands, accs, finished = {}, {}, {}, []
+        LAG = 2
+        sort_step(0)
+        for s in range(len(steps) + LAG):
+            if s < len(steps):
+                n, first = steps[s]
+                free_banks = [4, 5, 6, 7] if s < HEAD_GROUPS * (PASSES // RUN_PASSES) + LAG else [2, 3, 4, 5, 6, 7]
+                for c in range(first, first + RUN_PASSES):
+                    grouped[(n, c)] = transpose_pass(n, c, free_banks)
+                issue_loads(max(loads.index(key) for key in keys_of(s)) + 1 + AHEAD)
+            while finished:
+                done = finished.pop()
+                for pair in range(GROUP // (2 * P)):
+                    transpose_back(done, pair, free_banks)
+            if s + 1 < len(steps):
+                sort_step(s + 1)
+            new_chunk = s < len(steps) and steps[s][0] == 0 and steps[s][1] % LOAD_PASSES == 0
+            if new_chunk:
+                w_grouped = prepare_weights(first // LOAD_PASSES, None)
+            if 0 < s <= len(steps):
+                n, first = steps[s - 1]
+                for c in range(first, first + RUN_PASSES):
+                    operands[(n, c)] = quantise_pass(grouped[(n, c)])
+            if new_chunk:
+                quantise_weights(w_grouped, steps[s][1] // LOAD_PASSES)
+            if s >= LAG:
+                n, first = steps[s - LAG]
+                if first == 0:
+                    accs[n] = [psum.tile([P, GROUP], F32, name="bank%d" % acc_banks[n][m]) for m in range(M_TILES)]
+                for c in range(first, first + RUN_PASSES):
+                    multiply_pass(operands[(n, c)], c, accs[n])
+                if first + RUN_PASSES == PASSES:
+                    if s == len(steps) + LAG - 1:
+                        for pair in range(GROUP // (2 * P)):
+                            shift_out_of_psum(n, accs[n], pair * 2 * P, (pair + 1) * 2 * P)
+                        for pair in range(GROUP // (2 * P)):
+                            transpose_back(n, pair, free_banks)
+                    else:
+                        shift_out_of_psum(n, accs[n], 0, GROUP)
+                        finished.append(n)

@@ -20,15 +20,24 @@ WORDS = K_PASS // 2
 PASSES = D_OUT // K_PASS
 GROUP = 512
 GROUPS = TOKENS // GROUP
+TILES = GROUP // P
 M_TILES = D_IN // P
 
-LOAD_PASSES = 4
-LOAD_K = LOAD_PASSES * K_PASS
-CHUNKS = PASSES // LOAD_PASSES
+STEP_PASSES = 2
+STEP_K = STEP_PASSES * K_PASS
+STEPS = PASSES // STEP_PASSES
+ROWS = TILES * STEP_PASSES
 PAIR = 2
-PAIRS = GROUP // (PAIR * P)
-SORTED = 6
-RUN_PASSES = 2
+
+HEAD_GROUPS = 2
+HEAD_ROWS = 4, 1
+LATER_ROWS = 8, 0
+PLAIN_STEPS = 4
+SORT_AHEAD = 1
+QUANTISE_LAG = 1
+LAG = 2
+W_LAG = 0
+AHEAD = 12
 
 FLOPS = 2 * TOKENS * D_OUT * D_IN
 BYTES = 2 * TOKENS * D_OUT + 2 * D_OUT * D_IN + 4 * TOKENS * D_IN
@@ -41,10 +50,10 @@ def tile_relativemultiheadattention_pa_k_kernel(tc, pos_embed, W_r, b_r, grad_ou
 
     with ExitStack() as ctx:
         keep = ctx.enter_context(tc.tile_pool(name="keep", bufs=1))
-        grad_pool = ctx.enter_context(tc.tile_pool(name="grad", bufs=8))
-        w_raw_pool = ctx.enter_context(tc.tile_pool(name="w_raw", bufs=3))
-        w_grouped_pool = ctx.enter_context(tc.tile_pool(name="w_grouped", bufs=2))
-        ordered_pool = ctx.enter_context(tc.tile_pool(name="ordered", bufs=5))
+        grad_pool = ctx.enter_context(tc.tile_pool(name="grad", bufs=9))
+        w_raw_pool = ctx.enter_context(tc.tile_pool(name="w_raw", bufs=4))
+        w_grouped_pool = ctx.enter_context(tc.tile_pool(name="w_grouped", bufs=3))
+        ordered_pool = ctx.enter_context(tc.tile_pool(name="ordered", bufs=3))
         grouped_pool = ctx.enter_context(tc.tile_pool(name="grouped", bufs=6))
         operand_pool = ctx.enter_context(tc.tile_pool(name="operand", bufs=10))
         result_pool = ctx.enter_context(tc.tile_pool(name="result", bufs=4))
@@ -61,103 +70,140 @@ def tile_relativemultiheadattention_pa_k_kernel(tc, pos_embed, W_r, b_r, grad_ou
         for m in range(M_TILES):
             nc.vector.memset(g_t[m][:, 0:8], 0.0)
 
-        raws, w_raws = {}, {}
+        steps = [(n, q) for q in range(STEPS) for n in range(HEAD_GROUPS)]
+        steps += [(n, q) for n in range(HEAD_GROUPS, GROUPS) for q in range(STEPS)]
+        raws, ordered, ordered_too, w_raws, w_grouped = {}, {}, {}, {}, {}
+        grouped, operands, accs = {}, {}, {}
 
-        def load_grad(n, pair, chunk):
-            raw = grad_pool.tile([P, PAIR, LOAD_PASSES, K_PASS], BF16, name="grad_raw")
-            row0 = n * GROUP + pair * PAIR * P
-            rows = grad_rows[row0 : row0 + PAIR * P, chunk * LOAD_K : (chunk + 1) * LOAD_K]
-            nc.sync.dma_start(
-                out=raw[:].rearrange("p s g k -> p s (g k)"),
-                in_=rows.rearrange("(s p) k -> p s k", p=P),
-            )
-            raws[(n, pair, chunk)] = raw
+        def load_grad(s):
+            n, q = steps[s]
+            raw = grad_pool.tile([P, TILES, STEP_PASSES, K_PASS], BF16, name="grad_raw")
+            pieces = 2 if s == 0 else 1
+            size = TILES // pieces
+            for i in range(0, TILES, size):
+                row0 = n * GROUP + i * P
+                rows = grad_rows[row0 : row0 + size * P, q * STEP_K : (q + 1) * STEP_K]
+                nc.sync.dma_start(
+                    out=raw[:, i : i + size, :, :].rearrange("p s g k -> p s (g k)"),
+                    in_=rows.rearrange("(s p) k -> p s k", p=P),
+                )
+            raws[s] = raw
 
-        def load_weights(chunk):
-            raw = w_raw_pool.tile([P, LOAD_PASSES, PACK, D_IN], BF16, name="w_raw")
-            rows = W_r[chunk * LOAD_K : (chunk + 1) * LOAD_K, :]
+        def load_weights(q):
+            w_raw = w_raw_pool.tile([P, STEP_PASSES, PACK, D_IN], BF16, name="w_raw")
+            rows = W_r[q * STEP_K : (q + 1) * STEP_K, :]
             nc.sync.dma_start(
-                out=raw[:].rearrange("p g t d -> p g (t d)"),
+                out=w_raw[:].rearrange("p g t d -> p g (t d)"),
                 in_=rows.rearrange("(g p t) d -> p g (t d)", p=P, t=PACK),
             )
-            w_raws[chunk] = raw
+            w_raws[q] = w_raw
 
-        def prepare_weights(chunk, passes):
-            raw = w_raws[chunk]
-            grouped = w_grouped_pool.tile([P, LOAD_PASSES, D_IN, PACK], BF16, name="w_grouped", align_bytes=64)
-            for j in range(LOAD_PASSES):
-                nc.vector.tensor_copy(
-                    out=grouped[:, j, :, :].rearrange("p (c i) t -> p c t i", i=4),
-                    in_=raw[:, j, :, :].rearrange("p t (c i) -> p c t i", i=4),
-                )
-            return grouped
+        loads = []
+        for s in range(len(steps)):
+            loads.append((load_grad, s))
+            q, odd = divmod(s - W_LAG, HEAD_GROUPS)
+            if odd == 0 and 0 <= q < STEPS:
+                loads.append((load_weights, q))
+        issued = [0]
 
-        def quantise_weights(grouped, chunk):
-            passes = slice(chunk * LOAD_PASSES, (chunk + 1) * LOAD_PASSES)
+        def issue_loads(count):
+            while issued[0] < min(count, len(loads)):
+                load, index = loads[issued[0]]
+                issued[0] += 1
+                load(index)
+
+        def regroup_weights(c):
+            q, g = divmod(c, STEP_PASSES)
+            tile = w_grouped_pool.tile([P, D_IN, PACK], BF16, name="w_grouped", align_bytes=64)
+            nc.vector.tensor_copy(
+                out=tile[:].rearrange("p (c i) t -> p c t i", i=4),
+                in_=w_raws[q][:, g, :, :].rearrange("p t (c i) -> p c t i", i=4),
+            )
+            w_grouped[c] = tile
+
+        def quantise_weights(c):
             nc.vector.quantize_mx(
-                out=w_codes[:, passes, :].rearrange("p c d -> p (c d)").bitcast(E4M3X4),
-                scales=w_scales[:, passes, :].rearrange("p c d -> p (c d)"),
-                in_=grouped[:].rearrange("p c d t -> p (c d t)"),
+                out=w_codes[:, c, :].bitcast(E4M3X4),
+                scales=w_scales[:, c, :],
+                in_=w_grouped[c][:].rearrange("p d t -> p (d t)"),
             )
 
-        ordered = {}
+        def sorted_rows(s):
+            if s < PLAIN_STEPS:
+                return 0, 0
+            return HEAD_ROWS if s < HEAD_GROUPS * STEPS else LATER_ROWS
 
-        def sort_words(key):
-            if SORTED > 0:
-                tile = ordered_pool.tile([P, SORTED, 2, P], F32, name="ordered")
-                rows = raws[key][:].rearrange("p s g k -> p (s g) k")[:, 0:SORTED, :]
+        def sort_step(s):
+            vector_rows, scalar_rows = sorted_rows(s)
+            rows = raws[s][:].rearrange("p s g k -> p (s g) k").bitcast(F32)
+            if vector_rows > 0:
+                ordered[s] = ordered_pool.tile([P, ROWS, 2, P], F32, name="ordered")
                 nc.vector.tensor_copy(
-                    out=tile[:],
-                    in_=rows.bitcast(F32).rearrange("p x (j u) -> p x u j", u=2),
+                    out=ordered[s][:, 0:vector_rows, :, :],
+                    in_=rows[:, 0:vector_rows, :].rearrange("p x (j u) -> p x u j", u=2),
                 )
-                ordered[key] = tile
+            if scalar_rows > 0:
+                ordered_too[s] = ordered_pool.tile([P, scalar_rows, 2, P], F32, name="ordered_too")
+                nc.scalar.copy(
+                    out=ordered_too[s][:],
+                    in_=rows[:, vector_rows : vector_rows + scalar_rows, :].rearrange("p x (j u) -> p x u j", u=2),
+                )
 
-        def words_of(key, s, c, u):
-            x = s * LOAD_PASSES + c
-            if x < SORTED:
-                return ordered[key][:, x, u, :]
-            return raws[key][:, s, c, :].bitcast(F32)[:, u:WORDS:2]
+        def words_of(s, tile, g, u):
+            x = tile * STEP_PASSES + g
+            vector_rows, scalar_rows = sorted_rows(s)
+            if x < vector_rows:
+                return ordered[s][:, x, u, :]
+            if x < vector_rows + scalar_rows:
+                return ordered_too[s][:, x - vector_rows, u, :]
+            return raws[s][:, tile, g, :].bitcast(F32)[:, u:WORDS:2]
 
         bank_turn = [0]
 
-        def transpose_pass(n, c, banks):
-            grouped = grouped_pool.tile([P, GROUP, PACK], BF16, name="grouped", align_bytes=64)
-            chunk, c_in = divmod(c, LOAD_PASSES)
-            for pair in range(PAIRS):
-                bank = psum.tile([P, 2, PAIR * P], F32, name="bank%d" % banks[bank_turn[0] % len(banks)])
-                bank_turn[0] += 1
-                for s in range(PAIR):
-                    for u in range(2):
-                        nc.tensor.transpose(
-                            bank[:, u, s * P : (s + 1) * P],
-                            words_of((n, pair, chunk), s, c_in, u),
-                            identity[:],
-                        )
-                words = (
-                    grouped[:, pair * PAIR * P : (pair + 1) * PAIR * P, :]
-                    .rearrange("p r t -> p (r t)")
-                    .bitcast(F32)
-                    .rearrange("p (r u) -> p r u", u=2)
-                )
-                nc.scalar.copy(out=words, in_=bank[:].rearrange("p u r -> p r u"))
-            return grouped
+        def next_bank(shape, banks):
+            bank_turn[0] += 1
+            return psum.tile(shape, F32, name="bank%d" % banks[bank_turn[0] % len(banks)])
 
-        def quantise_pass(grouped):
+        def transpose_step(s, banks):
+            for g in range(STEP_PASSES):
+                tile = grouped_pool.tile([P, GROUP, PACK], BF16, name="grouped", align_bytes=64)
+                grouped[(s, g)] = tile
+                for first in range(0, TILES, PAIR):
+                    bank = next_bank([P, 2, PAIR * P], banks)
+                    for i in range(PAIR):
+                        for u in range(2):
+                            nc.tensor.transpose(
+                                bank[:, u, i * P : (i + 1) * P], words_of(s, first + i, g, u), identity[:]
+                            )
+                    words = (
+                        tile[:, first * P : (first + PAIR) * P, :]
+                        .rearrange("p r t -> p (r t)")
+                        .bitcast(F32)
+                        .rearrange("p (r u) -> p r u", u=2)
+                    )
+                    nc.scalar.copy(out=words, in_=bank[:].rearrange("p u r -> p r u"))
+
+        def quantise_pass(s, g):
             codes = operand_pool.tile([P, GROUP], U32, name="grad_codes", align_bytes=64)
             scales = operand_pool.tile([P, GROUP], U8, name="grad_scales", align_bytes=64)
             nc.vector.quantize_mx(
                 out=codes[:].bitcast(E5M2X4),
                 scales=scales[:],
-                in_=grouped[:].rearrange("p r t -> p (r t)"),
+                in_=grouped[(s, g)][:].rearrange("p r t -> p (r t)"),
             )
-            return codes, scales
+            operands[(s, g)] = codes, scales
 
-        def multiply_pass(operand, c, acc):
-            codes, scales = operand
-            for m in range(M_TILES):
+        def multiply_step(s, only=tuple(range(M_TILES))):
+            n, q = steps[s]
+            if n not in accs:
+                first_bank = M_TILES * (n % HEAD_GROUPS)
+                accs[n] = [psum.tile([P, GROUP], F32, name="bank%d" % (first_bank + m)) for m in range(M_TILES)]
+            for g, m in [(g, m) for g in range(STEP_PASSES) for m in only]:
+                codes, scales = operands[(s, g)]
+                c = q * STEP_PASSES + g
                 columns = slice(m * P, (m + 1) * P)
                 nc.tensor.matmul_mx(
-                    out=acc[m][:],
+                    out=accs[n][m][:],
                     lhsT=w_codes[:, c, columns].bitcast(E4M3X4),
                     lhsT_scale=w_scales[:, c, columns],
                     rhs=codes[:].bitcast(E5M2X4),
@@ -166,117 +212,92 @@ def tile_relativemultiheadattention_pa_k_kernel(tc, pos_embed, W_r, b_r, grad_ou
                     stop=(c == PASSES - 1),
                 )
 
-        def shift_out_of_psum(n, acc, first, last):
-            for m in range(M_TILES):
-                for b in range(BATCH):
-                    lo = max((SEQ + 1) * b - 2, n * GROUP + first)
-                    hi = min((SEQ + 1) * b - 2 + SEQ, n * GROUP + last)
-                    if lo < hi:
-                        src = acc[m][:, lo - n * GROUP : hi - n * GROUP]
-                        dst = g_t[m][:, lo + 2 - b : hi + 2 - b]
-                        if m == 0:
-                            nc.scalar.copy(out=dst, in_=src)
-                        else:
-                            nc.vector.tensor_copy(out=dst, in_=src)
-
-        def transpose_back(n, pair, banks):
-            row0 = n * GROUP + pair * 2 * P
-            bank = psum.tile([P, 2, D_IN], F32, name="bank%d" % banks[bank_turn[0] % len(banks)])
-            bank_turn[0] += 1
-            for j in range(2):
-                for m in range(M_TILES):
-                    nc.tensor.transpose(
-                        bank[:, j, m * P : (m + 1) * P],
-                        g_t[m][:, row0 + j * P : row0 + (j + 1) * P],
-                        identity[:],
+        def shift_out_of_psum(n, m, first, last, copy):
+            for b in range(BATCH):
+                lo = max((SEQ + 1) * b - 2, n * GROUP + first)
+                hi = min((SEQ + 1) * b - 2 + SEQ, n * GROUP + last)
+                if lo < hi:
+                    copy(
+                        out=g_t[m][:, lo + 2 - b : hi + 2 - b],
+                        in_=accs[n][m][:, lo - n * GROUP : hi - n * GROUP],
                     )
-            result = result_pool.tile([P, 2, D_IN], F32, name="result")
-            if pair == 0:
-                nc.scalar.copy(out=result[:], in_=bank[:])
-            else:
-                nc.vector.tensor_copy(out=result[:], in_=bank[:])
+
+        def transpose_half_back(n, m, tiles, banks, copy):
+            bank = next_bank([P, len(tiles), P], banks)
+            for j, tile in enumerate(tiles):
+                row0 = n * GROUP + tile * P
+                nc.tensor.transpose(bank[:, j, :], g_t[m][:, row0 : row0 + P], identity[:])
+            result = result_pool.tile([P, TILES, P], F32, name="result_half")
+            copy(out=result[:, 0 : len(tiles), :], in_=bank[:])
+            row0 = n * GROUP + tiles[0] * P
             nc.sync.dma_start(
-                out=out_rows[row0 : row0 + 2 * P, :].rearrange("(j p) d -> p j d", p=P),
-                in_=result[:],
+                out=out_rows[row0 : row0 + len(tiles) * P, m * P : (m + 1) * P].rearrange("(j p) d -> p j d", p=P),
+                in_=result[:, 0 : len(tiles), :],
             )
 
-        HEAD_GROUPS = 2
-        loads = []
-        steps = []
-        for chunk in range(CHUNKS):
-            for n in range(HEAD_GROUPS):
-                loads += [(n, pair, chunk) for pair in range(PAIRS)]
-                if n == 0:
-                    loads.append(chunk)
-            for first in range(0, LOAD_PASSES, RUN_PASSES):
-                for n in range(HEAD_GROUPS):
-                    steps.append((n, chunk * LOAD_PASSES + first))
-        for n in range(HEAD_GROUPS, GROUPS):
-            for chunk in range(CHUNKS):
-                loads += [(n, pair, chunk) for pair in range(PAIRS)]
-                for first in range(0, LOAD_PASSES, RUN_PASSES):
-                    steps.append((n, chunk * LOAD_PASSES + first))
-        acc_banks = {0: (0, 1), 1: (2, 3), 2: (0, 1)}
-
-        AHEAD = 8
-        issued = [0]
-
-        def issue_loads(count):
-            while issued[0] < min(count, len(loads)):
-                item = loads[issued[0]]
-                issued[0] += 1
-                if item in range(CHUNKS):
-                    load_weights(item)
+        def transpose_back(n, banks):
+            for first in range(0, TILES, PAIR):
+                row0 = n * GROUP + first * P
+                bank = next_bank([P, PAIR, D_IN], banks)
+                for j in range(PAIR):
+                    for m in range(M_TILES):
+                        nc.tensor.transpose(
+                            bank[:, j, m * P : (m + 1) * P],
+                            g_t[m][:, row0 + j * P : row0 + (j + 1) * P],
+                            identity[:],
+                        )
+                result = result_pool.tile([P, PAIR, D_IN], F32, name="result")
+                if False:
+                    nc.vector.tensor_copy(out=result[:], in_=bank[:])
                 else:
-                    load_grad(*item)
-
-        def keys_of(s):
-            n, first = steps[s]
-            return [(n, pair, first // LOAD_PASSES) for pair in range(PAIRS)]
-
-        def sort_step(s):
-            for key in keys_of(s):
-                if key not in ordered:
-                    sort_words(key)
+                    nc.scalar.copy(out=result[:], in_=bank[:])
+                nc.sync.dma_start(
+                    out=out_rows[row0 : row0 + PAIR * P, :].rearrange("(j p) d -> p j d", p=P),
+                    in_=result[:],
+                )
 
         issue_loads(AHEAD)
-        grouped, operands, accs, finished = {}, {}, {}, []
-        LAG = 2
-        sort_step(0)
-        for s in range(len(steps) + LAG):
-            if s < len(steps):
-                n, first = steps[s]
-                free_banks = [4, 5, 6, 7] if s < HEAD_GROUPS * (PASSES // RUN_PASSES) + LAG else [2, 3, 4, 5, 6, 7]
-                for c in range(first, first + RUN_PASSES):
-                    grouped[(n, c)] = transpose_pass(n, c, free_banks)
-                issue_loads(max(loads.index(key) for key in keys_of(s)) + 1 + AHEAD)
+        for s in range(SORT_AHEAD):
+            sort_step(s)
+        finished = []
+        for s in range(len(steps)):
+            head = s < HEAD_GROUPS * STEPS + LAG
+            free_banks = list(range(M_TILES * (HEAD_GROUPS if head else 1), 8))
+            q, g = divmod(s - W_LAG, STEP_PASSES)
+            weights = [q * STEP_PASSES + g] if 0 <= q < STEPS else []
+            for c in weights:
+                regroup_weights(c)
+            if s + SORT_AHEAD < len(steps):
+                sort_step(s + SORT_AHEAD)
+            transpose_step(s, free_banks)
+            issue_loads(loads.index((load_grad, s)) + 1 + AHEAD)
+            if s >= QUANTISE_LAG:
+                for g in range(STEP_PASSES):
+                    quantise_pass(s - QUANTISE_LAG, g)
+            for c in weights:
+                quantise_weights(c)
             while finished:
-                done = finished.pop()
-                for pair in range(GROUP // (2 * P)):
-                    transpose_back(done, pair, free_banks)
-            if s + 1 < len(steps):
-                sort_step(s + 1)
-            new_chunk = s < len(steps) and steps[s][0] == 0 and steps[s][1] % LOAD_PASSES == 0
-            if new_chunk:
-                w_grouped = prepare_weights(first // LOAD_PASSES, None)
-            if 0 < s <= len(steps):
-                n, first = steps[s - 1]
-                for c in range(first, first + RUN_PASSES):
-                    operands[(n, c)] = quantise_pass(grouped[(n, c)])
-            if new_chunk:
-                quantise_weights(w_grouped, steps[s][1] // LOAD_PASSES)
+                transpose_back(finished.pop(), free_banks)
             if s >= LAG:
-                n, first = steps[s - LAG]
-                if first == 0:
-                    accs[n] = [psum.tile([P, GROUP], F32, name="bank%d" % acc_banks[n][m]) for m in range(M_TILES)]
-                for c in range(first, first + RUN_PASSES):
-                    multiply_pass(operands[(n, c)], c, accs[n])
-                if first + RUN_PASSES == PASSES:
-                    if s == len(steps) + LAG - 1:
-                        for pair in range(GROUP // (2 * P)):
-                            shift_out_of_psum(n, accs[n], pair * 2 * P, (pair + 1) * 2 * P)
-                        for pair in range(GROUP // (2 * P)):
-                            transpose_back(n, pair, free_banks)
-                    else:
-                        shift_out_of_psum(n, accs[n], 0, GROUP)
-                        finished.append(n)
+                multiply_step(s - LAG)
+                n, q = steps[s - LAG]
+                if q == STEPS - 1:
+                    shift_out_of_psum(n, 0, 0, GROUP, nc.scalar.copy)
+                    shift_out_of_psum(n, 1, 0, GROUP, nc.vector.tensor_copy)
+                    finished.append(n)
+
+        last = GROUPS - 1
+        for s in range(len(steps) - QUANTISE_LAG, len(steps)):
+            for g in range(STEP_PASSES):
+                quantise_pass(s, g)
+        for m in range(M_TILES):
+            for s in range(len(steps) - LAG, len(steps)):
+                multiply_step(s, (m,))
+            if m == 0:
+                shift_out_of_psum(last, m, 0, GROUP, nc.scalar.copy)
+        halves = [list(range(first, first + PAIR)) for first in range(0, TILES, PAIR)]
+        for tiles in halves:
+            shift_out_of_psum(last, 1, tiles[0] * P, (tiles[-1] + 1) * P, nc.vector.tensor_copy)
+        transpose_half_back(last, 0, list(range(TILES)), free_banks, nc.scalar.copy)
+        for tiles, copy in zip(halves, (nc.scalar.copy, nc.vector.tensor_copy)):
+            transpose_half_back(last, 1, tiles, free_banks, copy)

@@ -22,22 +22,27 @@ GROUP = 512
 GROUPS = TOKENS // GROUP
 TILES = GROUP // P
 M_TILES = D_IN // P
-
-STEP_PASSES = 2
-STEP_K = STEP_PASSES * K_PASS
-STEPS = PASSES // STEP_PASSES
-ROWS = TILES * STEP_PASSES
 PAIR = 2
 
+ROWS = 8
+W_PASSES = 2
 HEAD_GROUPS = 2
-HEAD_ROWS = 4, 1
-LATER_ROWS = 8, 0
-PLAIN_STEPS = 4
-SORT_AHEAD = 1
-QUANTISE_LAG = 1
-LAG = 2
+HEAD_LOADS = HEAD_GROUPS * PASSES * TILES // ROWS
+PLAIN_LOADS = 4
+HEAD_SORT = 4, 0
+LATER_SORT = 7, 0
+MIDDLE_LOADS = 0
+MIDDLE_BANKS = (3,)
+MIDDLE_SORT = 4, 0
+LAST_LOADS = 1
+LAST_BANKS = ()
+MULTIPLY_FIRST = 0
+RESULT_LAG = 1
 W_LAG = 0
+W_WORK_LAG = 0
+SORT_AHEAD = 1
 AHEAD = 12
+STEP_PASSES = 2
 
 FLOPS = 2 * TOKENS * D_OUT * D_IN
 BYTES = 2 * TOKENS * D_OUT + 2 * D_OUT * D_IN + 4 * TOKENS * D_IN
@@ -54,7 +59,7 @@ def tile_relativemultiheadattention_pa_k_kernel(tc, pos_embed, W_r, b_r, grad_ou
         w_raw_pool = ctx.enter_context(tc.tile_pool(name="w_raw", bufs=4))
         w_grouped_pool = ctx.enter_context(tc.tile_pool(name="w_grouped", bufs=3))
         ordered_pool = ctx.enter_context(tc.tile_pool(name="ordered", bufs=3))
-        grouped_pool = ctx.enter_context(tc.tile_pool(name="grouped", bufs=6))
+        grouped_pool = ctx.enter_context(tc.tile_pool(name="grouped", bufs=9))
         operand_pool = ctx.enter_context(tc.tile_pool(name="operand", bufs=10))
         result_pool = ctx.enter_context(tc.tile_pool(name="result", bufs=4))
         psum = ctx.enter_context(tc.psum_pool(name="psum", bufs=1))
@@ -70,40 +75,43 @@ def tile_relativemultiheadattention_pa_k_kernel(tc, pos_embed, W_r, b_r, grad_ou
         for m in range(M_TILES):
             nc.vector.memset(g_t[m][:, 0:8], 0.0)
 
-        steps = [(n, q) for q in range(STEPS) for n in range(HEAD_GROUPS)]
-        steps += [(n, q) for n in range(HEAD_GROUPS, GROUPS) for q in range(STEPS)]
-        raws, ordered, ordered_too, w_raws, w_grouped = {}, {}, {}, {}, {}
-        grouped, operands, accs = {}, {}, {}
+        grads = []
+        for c in range(0, PASSES, 2):
+            grads += [(n, 0, TILES, c, 2) for n in range(HEAD_GROUPS)]
+        for n in range(HEAD_GROUPS, GROUPS):
+            grads += [(n, 0, TILES, c, 2) for c in range(0, PASSES, 2)]
 
-        def load_grad(s):
-            n, q = steps[s]
-            raw = grad_pool.tile([P, TILES, STEP_PASSES, K_PASS], BF16, name="grad_raw")
-            pieces = 2 if s == 0 else 1
-            size = TILES // pieces
-            for i in range(0, TILES, size):
-                row0 = n * GROUP + i * P
-                rows = grad_rows[row0 : row0 + size * P, q * STEP_K : (q + 1) * STEP_K]
+        raws, w_raws = {}, {}
+
+        def load_grad(i):
+            n, tile, tiles, c, passes = grads[i]
+            raw = grad_pool.tile([P, tiles, passes, K_PASS], BF16, name="grad_raw")
+            size = PAIR if i == 0 else tiles
+            for first in range(0, tiles, size):
+                row0 = n * GROUP + (tile + first) * P
+                rows = grad_rows[row0 : row0 + size * P, c * K_PASS : (c + passes) * K_PASS]
                 nc.sync.dma_start(
-                    out=raw[:, i : i + size, :, :].rearrange("p s g k -> p s (g k)"),
+                    out=raw[:, first : first + size, :, :].rearrange("p s g k -> p s (g k)"),
                     in_=rows.rearrange("(s p) k -> p s k", p=P),
                 )
-            raws[s] = raw
+            raws[i] = raw
 
-        def load_weights(q):
-            w_raw = w_raw_pool.tile([P, STEP_PASSES, PACK, D_IN], BF16, name="w_raw")
-            rows = W_r[q * STEP_K : (q + 1) * STEP_K, :]
+        def load_weights(c):
+            w_raw = w_raw_pool.tile([P, W_PASSES, PACK, D_IN], BF16, name="w_raw")
+            rows = W_r[c * K_PASS : (c + W_PASSES) * K_PASS, :]
             nc.sync.dma_start(
                 out=w_raw[:].rearrange("p g t d -> p g (t d)"),
                 in_=rows.rearrange("(g p t) d -> p g (t d)", p=P, t=PACK),
             )
-            w_raws[q] = w_raw
+            for g in range(W_PASSES):
+                w_raws[c + g] = w_raw[:, g, :, :]
 
         loads = []
-        for s in range(len(steps)):
-            loads.append((load_grad, s))
-            q, odd = divmod(s - W_LAG, HEAD_GROUPS)
-            if odd == 0 and 0 <= q < STEPS:
-                loads.append((load_weights, q))
+        for i in range(len(grads)):
+            loads.append((load_grad, i))
+            c = i - W_LAG
+            if 0 <= c < PASSES and c % W_PASSES == 0:
+                loads.append((load_weights, c))
         issued = [0]
 
         def issue_loads(count):
@@ -112,12 +120,13 @@ def tile_relativemultiheadattention_pa_k_kernel(tc, pos_embed, W_r, b_r, grad_ou
                 issued[0] += 1
                 load(index)
 
+        w_grouped = {}
+
         def regroup_weights(c):
-            q, g = divmod(c, STEP_PASSES)
             tile = w_grouped_pool.tile([P, D_IN, PACK], BF16, name="w_grouped", align_bytes=64)
             nc.vector.tensor_copy(
                 out=tile[:].rearrange("p (c i) t -> p c t i", i=4),
-                in_=w_raws[q][:, g, :, :].rearrange("p t (c i) -> p c t i", i=4),
+                in_=w_raws[c].rearrange("p t (c i) -> p c t i", i=4),
             )
             w_grouped[c] = tile
 
@@ -128,89 +137,116 @@ def tile_relativemultiheadattention_pa_k_kernel(tc, pos_embed, W_r, b_r, grad_ou
                 in_=w_grouped[c][:].rearrange("p d t -> p (d t)"),
             )
 
-        def sorted_rows(s):
-            if s < PLAIN_STEPS:
-                return 0, 0
-            return HEAD_ROWS if s < HEAD_GROUPS * STEPS else LATER_ROWS
+        ordered, ordered_too = {}, {}
 
-        def sort_step(s):
-            vector_rows, scalar_rows = sorted_rows(s)
-            rows = raws[s][:].rearrange("p s g k -> p (s g) k").bitcast(F32)
+        def sorted_rows(i):
+            if i < PLAIN_LOADS:
+                return 0, 0
+            if i >= len(grads) - 1:
+                return 8, 0
+            if HEAD_LOADS <= i < HEAD_LOADS + MIDDLE_LOADS:
+                return MIDDLE_SORT
+            return HEAD_SORT if i < HEAD_LOADS else LATER_SORT
+
+        def sort_words(i):
+            vector_rows, scalar_rows = sorted_rows(i)
+            rows = raws[i][:].rearrange("p s g k -> p (s g) k").bitcast(F32)
             if vector_rows > 0:
-                ordered[s] = ordered_pool.tile([P, ROWS, 2, P], F32, name="ordered")
+                ordered[i] = ordered_pool.tile([P, ROWS, 2, P], F32, name="ordered")
                 nc.vector.tensor_copy(
-                    out=ordered[s][:, 0:vector_rows, :, :],
+                    out=ordered[i][:, 0:vector_rows, :, :],
                     in_=rows[:, 0:vector_rows, :].rearrange("p x (j u) -> p x u j", u=2),
                 )
             if scalar_rows > 0:
-                ordered_too[s] = ordered_pool.tile([P, scalar_rows, 2, P], F32, name="ordered_too")
+                ordered_too[i] = ordered_pool.tile([P, scalar_rows, 2, P], F32, name="ordered_too")
                 nc.scalar.copy(
-                    out=ordered_too[s][:],
+                    out=ordered_too[i][:],
                     in_=rows[:, vector_rows : vector_rows + scalar_rows, :].rearrange("p x (j u) -> p x u j", u=2),
                 )
 
-        def words_of(s, tile, g, u):
-            x = tile * STEP_PASSES + g
-            vector_rows, scalar_rows = sorted_rows(s)
-            if x < vector_rows:
-                return ordered[s][:, x, u, :]
-            if x < vector_rows + scalar_rows:
-                return ordered_too[s][:, x - vector_rows, u, :]
-            return raws[s][:, tile, g, :].bitcast(F32)[:, u:WORDS:2]
+        def words_of(i, tile, g, u):
+            vector_rows, scalar_rows = sorted_rows(i)
+            row = tile * grads[i][4] + g
+            if row < vector_rows:
+                return ordered[i][:, row, u, :]
+            if row < vector_rows + scalar_rows:
+                return ordered_too[i][:, row - vector_rows, u, :]
+            return raws[i][:, tile, g, :].bitcast(F32)[:, u:WORDS:2]
 
+        grouped, operands, accs = {}, {}, {}
+        filled = {}
+        complete = []
         bank_turn = [0]
 
         def next_bank(shape, banks):
             bank_turn[0] += 1
             return psum.tile(shape, F32, name="bank%d" % banks[bank_turn[0] % len(banks)])
 
-        def transpose_step(s, banks):
-            for g in range(STEP_PASSES):
-                tile = grouped_pool.tile([P, GROUP, PACK], BF16, name="grouped", align_bytes=64)
-                grouped[(s, g)] = tile
-                for first in range(0, TILES, PAIR):
+        def vector_banks(i):
+            if i >= len(grads) - LAST_LOADS:
+                return LAST_BANKS
+            if HEAD_LOADS <= i < HEAD_LOADS + MIDDLE_LOADS:
+                return MIDDLE_BANKS
+            return ()
+
+        for_vector = []
+
+        def transpose_load(i, banks):
+            n, tile, tiles, first_pass, passes = grads[i]
+            bank_of_load = 0
+            for g in range(passes):
+                key = (n, first_pass + g)
+                if key not in grouped:
+                    grouped[key] = grouped_pool.tile([P, GROUP, PACK], BF16, name="grouped", align_bytes=64)
+                for first in range(0, tiles, PAIR):
                     bank = next_bank([P, 2, PAIR * P], banks)
-                    for i in range(PAIR):
+                    for j in range(PAIR):
                         for u in range(2):
                             nc.tensor.transpose(
-                                bank[:, u, i * P : (i + 1) * P], words_of(s, first + i, g, u), identity[:]
+                                bank[:, u, j * P : (j + 1) * P], words_of(i, first + j, g, u), identity[:]
                             )
                     words = (
-                        tile[:, first * P : (first + PAIR) * P, :]
+                        grouped[key][:, (tile + first) * P : (tile + first + PAIR) * P, :]
                         .rearrange("p r t -> p (r t)")
                         .bitcast(F32)
                         .rearrange("p (r u) -> p r u", u=2)
                     )
-                    nc.scalar.copy(out=words, in_=bank[:].rearrange("p u r -> p r u"))
+                    source = bank[:].rearrange("p u r -> p r u")
+                    bank_of_load += 1
+                    if bank_of_load % 4 in vector_banks(i):
+                        for_vector.append((words, source))
+                    else:
+                        nc.scalar.copy(out=words, in_=source)
+                filled[key] = filled.get(key, 0) + tiles
+                if filled[key] == TILES:
+                    complete.append(key)
 
-        def quantise_pass(s, g):
+        def quantise_pass(key):
             codes = operand_pool.tile([P, GROUP], U32, name="grad_codes", align_bytes=64)
             scales = operand_pool.tile([P, GROUP], U8, name="grad_scales", align_bytes=64)
             nc.vector.quantize_mx(
                 out=codes[:].bitcast(E5M2X4),
                 scales=scales[:],
-                in_=grouped[(s, g)][:].rearrange("p r t -> p (r t)"),
+                in_=grouped[key][:].rearrange("p r t -> p (r t)"),
             )
-            operands[(s, g)] = codes, scales
+            operands[key] = codes, scales
 
-        def multiply_step(s, only=tuple(range(M_TILES))):
-            n, q = steps[s]
+        def multiply_pass(key, m):
+            n, c = key
             if n not in accs:
                 first_bank = M_TILES * (n % HEAD_GROUPS)
-                accs[n] = [psum.tile([P, GROUP], F32, name="bank%d" % (first_bank + m)) for m in range(M_TILES)]
-            for g, m in [(g, m) for g in range(STEP_PASSES) for m in only]:
-                codes, scales = operands[(s, g)]
-                c = q * STEP_PASSES + g
-                columns = slice(m * P, (m + 1) * P)
-                nc.tensor.matmul_mx(
-                    out=accs[n][m][:],
-                    lhsT=w_codes[:, c, columns].bitcast(E4M3X4),
-                    lhsT_scale=w_scales[:, c, columns],
-                    rhs=codes[:].bitcast(E5M2X4),
-                    rhs_scale=scales[:],
-                    start=(c == 0),
-                    stop=(c == PASSES - 1),
-                )
+                accs[n] = [psum.tile([P, GROUP], F32, name="bank%d" % (first_bank + j)) for j in range(M_TILES)]
+            codes, scales = operands[key]
+            columns = slice(m * P, (m + 1) * P)
+            nc.tensor.matmul_mx(
+                out=accs[n][m][:],
+                lhsT=w_codes[:, c, columns].bitcast(E4M3X4),
+                lhsT_scale=w_scales[:, c, columns],
+                rhs=codes[:].bitcast(E5M2X4),
+                rhs_scale=scales[:],
+                start=(c == 0),
+                stop=(c == PASSES - 1),
+            )
 
         def shift_out_of_psum(n, m, first, last, copy):
             for b in range(BATCH):
@@ -222,12 +258,12 @@ def tile_relativemultiheadattention_pa_k_kernel(tc, pos_embed, W_r, b_r, grad_ou
                         in_=accs[n][m][:, lo - n * GROUP : hi - n * GROUP],
                     )
 
-        def transpose_half_back(n, m, tiles, banks, copy):
+        def transpose_back(n, m, tiles, banks, copy):
             bank = next_bank([P, len(tiles), P], banks)
             for j, tile in enumerate(tiles):
                 row0 = n * GROUP + tile * P
                 nc.tensor.transpose(bank[:, j, :], g_t[m][:, row0 : row0 + P], identity[:])
-            result = result_pool.tile([P, TILES, P], F32, name="result_half")
+            result = result_pool.tile([P, TILES, P], F32, name="result")
             copy(out=result[:, 0 : len(tiles), :], in_=bank[:])
             row0 = n * GROUP + tiles[0] * P
             nc.sync.dma_start(
@@ -235,69 +271,64 @@ def tile_relativemultiheadattention_pa_k_kernel(tc, pos_embed, W_r, b_r, grad_ou
                 in_=result[:, 0 : len(tiles), :],
             )
 
-        def transpose_back(n, banks):
-            for first in range(0, TILES, PAIR):
-                row0 = n * GROUP + first * P
-                bank = next_bank([P, PAIR, D_IN], banks)
-                for j in range(PAIR):
-                    for m in range(M_TILES):
-                        nc.tensor.transpose(
-                            bank[:, j, m * P : (m + 1) * P],
-                            g_t[m][:, row0 + j * P : row0 + (j + 1) * P],
-                            identity[:],
-                        )
-                result = result_pool.tile([P, PAIR, D_IN], F32, name="result")
-                if False:
-                    nc.vector.tensor_copy(out=result[:], in_=bank[:])
-                else:
-                    nc.scalar.copy(out=result[:], in_=bank[:])
-                nc.sync.dma_start(
-                    out=out_rows[row0 : row0 + PAIR * P, :].rearrange("(j p) d -> p j d", p=P),
-                    in_=result[:],
-                )
-
         issue_loads(AHEAD)
-        for s in range(SORT_AHEAD):
-            sort_step(s)
+        for i in range(SORT_AHEAD):
+            sort_words(i)
+        quantised = 0
+        multiplied = 0
+        prepared = 0
         finished = []
-        for s in range(len(steps)):
-            head = s < HEAD_GROUPS * STEPS + LAG
-            free_banks = list(range(M_TILES * (HEAD_GROUPS if head else 1), 8))
-            q, g = divmod(s - W_LAG, STEP_PASSES)
-            weights = [q * STEP_PASSES + g] if 0 <= q < STEPS else []
-            for c in weights:
-                regroup_weights(c)
-            if s + SORT_AHEAD < len(steps):
-                sort_step(s + SORT_AHEAD)
-            transpose_step(s, free_banks)
-            issue_loads(loads.index((load_grad, s)) + 1 + AHEAD)
-            if s >= QUANTISE_LAG:
-                for g in range(STEP_PASSES):
-                    quantise_pass(s - QUANTISE_LAG, g)
-            for c in weights:
-                quantise_weights(c)
-            while finished:
-                transpose_back(finished.pop(), free_banks)
-            if s >= LAG:
-                multiply_step(s - LAG)
-                n, q = steps[s - LAG]
-                if q == STEPS - 1:
-                    shift_out_of_psum(n, 0, 0, GROUP, nc.scalar.copy)
-                    shift_out_of_psum(n, 1, 0, GROUP, nc.vector.tensor_copy)
-                    finished.append(n)
 
+        def multiply_passes(end, leave=False):
+            for n, c in complete[multiplied:end]:
+                for m in range(M_TILES):
+                    multiply_pass((n, c), m)
+                if c == PASSES - 1 and not leave:
+                    shift_out_of_psum(n, 0, 0, GROUP, nc.vector.tensor_copy)
+                    shift_out_of_psum(n, 1, 0, GROUP, nc.vector.tensor_copy)
+                    finished.extend((n, m, i) for m in range(M_TILES))
+
+        for i in range(len(grads)):
+            weights = i - W_WORK_LAG
+            if 0 <= weights < PASSES:
+                regroup_weights(weights)
+            if i + SORT_AHEAD < len(grads):
+                sort_words(i + SORT_AHEAD)
+            can_quantise = min(len(complete), quantised + STEP_PASSES)
+            can_multiply = multiplied
+            while can_multiply < min(quantised, multiplied + STEP_PASSES) and complete[can_multiply][1] < prepared:
+                can_multiply += 1
+            free_banks = list(range(M_TILES * (HEAD_GROUPS if multiplied < HEAD_GROUPS * PASSES else 1), 8))
+            if i < MULTIPLY_FIRST:
+                multiply_passes(can_multiply)
+                multiplied = can_multiply
+            transpose_load(i, free_banks)
+            issue_loads(loads.index((load_grad, i)) + 1 + AHEAD)
+            for key in complete[quantised:can_quantise]:
+                quantise_pass(key)
+            quantised = can_quantise
+            while for_vector:
+                words, source = for_vector.pop(0)
+                nc.vector.tensor_copy(out=words, in_=source)
+            if 0 <= weights < PASSES:
+                quantise_weights(weights)
+                prepared = weights + 1
+            if finished and finished[0][2] + RESULT_LAG <= i:
+                done, m, since = finished.pop(0)
+                transpose_back(done, m, list(range(TILES)), free_banks, (nc.scalar.copy, nc.vector.tensor_copy)[m])
+            if i >= MULTIPLY_FIRST:
+                multiply_passes(can_multiply)
+                multiplied = can_multiply
+
+        for key in complete[quantised:]:
+            quantise_pass(key)
+        multiply_passes(len(complete), leave=True)
         last = GROUPS - 1
-        for s in range(len(steps) - QUANTISE_LAG, len(steps)):
-            for g in range(STEP_PASSES):
-                quantise_pass(s, g)
-        for m in range(M_TILES):
-            for s in range(len(steps) - LAG, len(steps)):
-                multiply_step(s, (m,))
-            if m == 0:
-                shift_out_of_psum(last, m, 0, GROUP, nc.scalar.copy)
-        halves = [list(range(first, first + PAIR)) for first in range(0, TILES, PAIR)]
-        for tiles in halves:
-            shift_out_of_psum(last, 1, tiles[0] * P, (tiles[-1] + 1) * P, nc.vector.tensor_copy)
-        transpose_half_back(last, 0, list(range(TILES)), free_banks, nc.scalar.copy)
-        for tiles, copy in zip(halves, (nc.scalar.copy, nc.vector.tensor_copy)):
-            transpose_half_back(last, 1, tiles, free_banks, copy)
+        copies = (nc.scalar.copy, nc.vector.tensor_copy)
+        parts = [list(range(first, first + PAIR)) for first in range(0, TILES, PAIR)]
+        for tiles in parts:
+            for m in range(M_TILES):
+                shift_out_of_psum(last, m, tiles[0] * P, (tiles[-1] + 1) * P, copies[m])
+        for tiles in parts:
+            for m in range(M_TILES):
+                transpose_back(last, m, tiles, free_banks, copies[m])

@@ -24,25 +24,19 @@ TILES = GROUP // P
 M_TILES = D_IN // P
 PAIR = 2
 
-ROWS = 8
-W_PASSES = 2
-HEAD_GROUPS = 2
-HEAD_LOADS = HEAD_GROUPS * PASSES * TILES // ROWS
-PLAIN_LOADS = 4
-HEAD_SORT = 4, 0
-LATER_SORT = 7, 0
-MIDDLE_LOADS = 0
-MIDDLE_BANKS = (3,)
-MIDDLE_SORT = 4, 0
-LAST_LOADS = 1
-LAST_BANKS = ()
-MULTIPLY_FIRST = 0
-RESULT_LAG = 1
-W_LAG = 0
-W_WORK_LAG = 0
-SORT_AHEAD = 1
-AHEAD = 12
 STEP_PASSES = 2
+STEP_K = STEP_PASSES * K_PASS
+ROWS = TILES * STEP_PASSES
+HEAD_GROUPS = 2
+HEAD_STEPS = HEAD_GROUPS * PASSES // STEP_PASSES
+
+PLAIN_STEPS = 4
+BUSY_STEPS = HEAD_STEPS + 3
+BUSY_ROWS = 4
+FREE_ROWS = 8
+
+GRAD_BUFS = 9
+LOADS_AHEAD = 12
 
 FLOPS = 2 * TOKENS * D_OUT * D_IN
 BYTES = 2 * TOKENS * D_OUT + 2 * D_OUT * D_IN + 4 * TOKENS * D_IN
@@ -55,10 +49,10 @@ def tile_relativemultiheadattention_pa_k_kernel(tc, pos_embed, W_r, b_r, grad_ou
 
     with ExitStack() as ctx:
         keep = ctx.enter_context(tc.tile_pool(name="keep", bufs=1))
-        grad_pool = ctx.enter_context(tc.tile_pool(name="grad", bufs=9))
+        grad_pool = ctx.enter_context(tc.tile_pool(name="grad", bufs=GRAD_BUFS))
         w_raw_pool = ctx.enter_context(tc.tile_pool(name="w_raw", bufs=4))
         w_grouped_pool = ctx.enter_context(tc.tile_pool(name="w_grouped", bufs=3))
-        ordered_pool = ctx.enter_context(tc.tile_pool(name="ordered", bufs=3))
+        sorted_pool = ctx.enter_context(tc.tile_pool(name="sorted", bufs=3))
         grouped_pool = ctx.enter_context(tc.tile_pool(name="grouped", bufs=9))
         operand_pool = ctx.enter_context(tc.tile_pool(name="operand", bufs=10))
         result_pool = ctx.enter_context(tc.tile_pool(name="result", bufs=4))
@@ -75,21 +69,18 @@ def tile_relativemultiheadattention_pa_k_kernel(tc, pos_embed, W_r, b_r, grad_ou
         for m in range(M_TILES):
             nc.vector.memset(g_t[m][:, 0:8], 0.0)
 
-        grads = []
-        for c in range(0, PASSES, 2):
-            grads += [(n, 0, TILES, c, 2) for n in range(HEAD_GROUPS)]
-        for n in range(HEAD_GROUPS, GROUPS):
-            grads += [(n, 0, TILES, c, 2) for c in range(0, PASSES, 2)]
+        steps = [(n, c) for c in range(0, PASSES, STEP_PASSES) for n in range(HEAD_GROUPS)]
+        steps += [(n, c) for n in range(HEAD_GROUPS, GROUPS) for c in range(0, PASSES, STEP_PASSES)]
 
         raws, w_raws = {}, {}
 
         def load_grad(i):
-            n, tile, tiles, c, passes = grads[i]
-            raw = grad_pool.tile([P, tiles, passes, K_PASS], BF16, name="grad_raw")
-            size = PAIR if i == 0 else tiles
-            for first in range(0, tiles, size):
-                row0 = n * GROUP + (tile + first) * P
-                rows = grad_rows[row0 : row0 + size * P, c * K_PASS : (c + passes) * K_PASS]
+            n, c = steps[i]
+            raw = grad_pool.tile([P, TILES, STEP_PASSES, K_PASS], BF16, name="grad_raw")
+            size = PAIR if i == 0 else TILES
+            for first in range(0, TILES, size):
+                row0 = n * GROUP + first * P
+                rows = grad_rows[row0 : row0 + size * P, c * K_PASS : c * K_PASS + STEP_K]
                 nc.sync.dma_start(
                     out=raw[:, first : first + size, :, :].rearrange("p s g k -> p s (g k)"),
                     in_=rows.rearrange("(s p) k -> p s k", p=P),
@@ -97,28 +88,28 @@ def tile_relativemultiheadattention_pa_k_kernel(tc, pos_embed, W_r, b_r, grad_ou
             raws[i] = raw
 
         def load_weights(c):
-            w_raw = w_raw_pool.tile([P, W_PASSES, PACK, D_IN], BF16, name="w_raw")
-            rows = W_r[c * K_PASS : (c + W_PASSES) * K_PASS, :]
+            w_raw = w_raw_pool.tile([P, STEP_PASSES, PACK, D_IN], BF16, name="w_raw")
+            rows = W_r[c * K_PASS : c * K_PASS + STEP_K, :]
             nc.sync.dma_start(
                 out=w_raw[:].rearrange("p g t d -> p g (t d)"),
                 in_=rows.rearrange("(g p t) d -> p g (t d)", p=P, t=PACK),
             )
-            for g in range(W_PASSES):
+            for g in range(STEP_PASSES):
                 w_raws[c + g] = w_raw[:, g, :, :]
 
         loads = []
-        for i in range(len(grads)):
+        for i in range(len(steps)):
+            n, c = steps[i]
             loads.append((load_grad, i))
-            c = i - W_LAG
-            if 0 <= c < PASSES and c % W_PASSES == 0:
+            if n == 0:
                 loads.append((load_weights, c))
         issued = [0]
 
         def issue_loads(count):
             while issued[0] < min(count, len(loads)):
-                load, index = loads[issued[0]]
+                load, argument = loads[issued[0]]
                 issued[0] += 1
-                load(index)
+                load(argument)
 
         w_grouped = {}
 
@@ -134,119 +125,97 @@ def tile_relativemultiheadattention_pa_k_kernel(tc, pos_embed, W_r, b_r, grad_ou
             nc.vector.quantize_mx(
                 out=w_codes[:, c, :].bitcast(E4M3X4),
                 scales=w_scales[:, c, :],
-                in_=w_grouped[c][:].rearrange("p d t -> p (d t)"),
+                in_=w_grouped.pop(c)[:].rearrange("p d t -> p (d t)"),
             )
 
-        ordered, ordered_too = {}, {}
+        sorted_words = {}
 
         def sorted_rows(i):
-            if i < PLAIN_LOADS:
-                return 0, 0
-            if i >= len(grads) - 1:
-                return 8, 0
-            if HEAD_LOADS <= i < HEAD_LOADS + MIDDLE_LOADS:
-                return MIDDLE_SORT
-            return HEAD_SORT if i < HEAD_LOADS else LATER_SORT
+            if i < PLAIN_STEPS:
+                return 0
+            return BUSY_ROWS if i < BUSY_STEPS else FREE_ROWS
 
         def sort_words(i):
-            vector_rows, scalar_rows = sorted_rows(i)
-            rows = raws[i][:].rearrange("p s g k -> p (s g) k").bitcast(F32)
-            if vector_rows > 0:
-                ordered[i] = ordered_pool.tile([P, ROWS, 2, P], F32, name="ordered")
+            count = sorted_rows(i)
+            if count > 0:
+                rows = raws[i][:].rearrange("p s g k -> p (s g) k").bitcast(F32)
+                tile = sorted_pool.tile([P, ROWS, 2, P], F32, name="sorted_words")
                 nc.vector.tensor_copy(
-                    out=ordered[i][:, 0:vector_rows, :, :],
-                    in_=rows[:, 0:vector_rows, :].rearrange("p x (j u) -> p x u j", u=2),
+                    out=tile[:, 0:count, :, :],
+                    in_=rows[:, 0:count, :].rearrange("p x (j u) -> p x u j", u=2),
                 )
-            if scalar_rows > 0:
-                ordered_too[i] = ordered_pool.tile([P, scalar_rows, 2, P], F32, name="ordered_too")
-                nc.scalar.copy(
-                    out=ordered_too[i][:],
-                    in_=rows[:, vector_rows : vector_rows + scalar_rows, :].rearrange("p x (j u) -> p x u j", u=2),
-                )
+                sorted_words[i] = tile
 
         def words_of(i, tile, g, u):
-            vector_rows, scalar_rows = sorted_rows(i)
-            row = tile * grads[i][4] + g
-            if row < vector_rows:
-                return ordered[i][:, row, u, :]
-            if row < vector_rows + scalar_rows:
-                return ordered_too[i][:, row - vector_rows, u, :]
+            row = tile * STEP_PASSES + g
+            if row < sorted_rows(i):
+                return sorted_words[i][:, row, u, :]
             return raws[i][:, tile, g, :].bitcast(F32)[:, u:WORDS:2]
 
-        grouped, operands, accs = {}, {}, {}
-        filled = {}
-        complete = []
+        grouped, operands, sums = {}, {}, {}
+        banks_free = [0]
         bank_turn = [0]
 
-        def next_bank(shape, banks):
+        def next_bank(shape):
+            count = 8 - banks_free[0]
             bank_turn[0] += 1
-            return psum.tile(shape, F32, name="bank%d" % banks[bank_turn[0] % len(banks)])
+            return psum.tile(shape, F32, name="bank%d" % (banks_free[0] + bank_turn[0] % count))
 
-        def vector_banks(i):
-            if i >= len(grads) - LAST_LOADS:
-                return LAST_BANKS
-            if HEAD_LOADS <= i < HEAD_LOADS + MIDDLE_LOADS:
-                return MIDDLE_BANKS
-            return ()
-
-        for_vector = []
-
-        def transpose_load(i, banks):
-            n, tile, tiles, first_pass, passes = grads[i]
-            bank_of_load = 0
-            for g in range(passes):
-                key = (n, first_pass + g)
-                if key not in grouped:
-                    grouped[key] = grouped_pool.tile([P, GROUP, PACK], BF16, name="grouped", align_bytes=64)
-                for first in range(0, tiles, PAIR):
-                    bank = next_bank([P, 2, PAIR * P], banks)
+        def transpose_step(i):
+            left = []
+            for g in range(STEP_PASSES):
+                tile = grouped_pool.tile([P, GROUP, PACK], BF16, name="grouped", align_bytes=64)
+                grouped[(i, g)] = tile
+                for first in range(0, TILES, PAIR):
+                    bank = next_bank([P, 2, PAIR * P])
                     for j in range(PAIR):
                         for u in range(2):
                             nc.tensor.transpose(
                                 bank[:, u, j * P : (j + 1) * P], words_of(i, first + j, g, u), identity[:]
                             )
                     words = (
-                        grouped[key][:, (tile + first) * P : (tile + first + PAIR) * P, :]
+                        tile[:, first * P : (first + PAIR) * P, :]
                         .rearrange("p r t -> p (r t)")
                         .bitcast(F32)
                         .rearrange("p (r u) -> p r u", u=2)
                     )
                     source = bank[:].rearrange("p u r -> p r u")
-                    bank_of_load += 1
-                    if bank_of_load % 4 in vector_banks(i):
-                        for_vector.append((words, source))
+                    if i == len(steps) - 1 and (g, first) == (1, PAIR):
+                        left.append((words, source))
                     else:
                         nc.scalar.copy(out=words, in_=source)
-                filled[key] = filled.get(key, 0) + tiles
-                if filled[key] == TILES:
-                    complete.append(key)
+            return left
 
-        def quantise_pass(key):
-            codes = operand_pool.tile([P, GROUP], U32, name="grad_codes", align_bytes=64)
-            scales = operand_pool.tile([P, GROUP], U8, name="grad_scales", align_bytes=64)
-            nc.vector.quantize_mx(
-                out=codes[:].bitcast(E5M2X4),
-                scales=scales[:],
-                in_=grouped[key][:].rearrange("p r t -> p (r t)"),
-            )
-            operands[key] = codes, scales
+        def quantise_step(i):
+            for g in range(STEP_PASSES):
+                codes = operand_pool.tile([P, GROUP], U32, name="grad_codes", align_bytes=64)
+                scales = operand_pool.tile([P, GROUP], U8, name="grad_scales", align_bytes=64)
+                nc.vector.quantize_mx(
+                    out=codes[:].bitcast(E5M2X4),
+                    scales=scales[:],
+                    in_=grouped.pop((i, g))[:].rearrange("p r t -> p (r t)"),
+                )
+                operands[(i, g)] = codes, scales
 
-        def multiply_pass(key, m):
-            n, c = key
-            if n not in accs:
+        def multiply_step(i):
+            n, first_pass = steps[i]
+            if first_pass == 0:
                 first_bank = M_TILES * (n % HEAD_GROUPS)
-                accs[n] = [psum.tile([P, GROUP], F32, name="bank%d" % (first_bank + j)) for j in range(M_TILES)]
-            codes, scales = operands[key]
-            columns = slice(m * P, (m + 1) * P)
-            nc.tensor.matmul_mx(
-                out=accs[n][m][:],
-                lhsT=w_codes[:, c, columns].bitcast(E4M3X4),
-                lhsT_scale=w_scales[:, c, columns],
-                rhs=codes[:].bitcast(E5M2X4),
-                rhs_scale=scales[:],
-                start=(c == 0),
-                stop=(c == PASSES - 1),
-            )
+                sums[n] = [psum.tile([P, GROUP], F32, name="bank%d" % (first_bank + m)) for m in range(M_TILES)]
+            for g in range(STEP_PASSES):
+                codes, scales = operands.pop((i, g))
+                c = first_pass + g
+                for m in range(M_TILES):
+                    columns = slice(m * P, (m + 1) * P)
+                    nc.tensor.matmul_mx(
+                        out=sums[n][m][:],
+                        lhsT=w_codes[:, c, columns].bitcast(E4M3X4),
+                        lhsT_scale=w_scales[:, c, columns],
+                        rhs=codes[:].bitcast(E5M2X4),
+                        rhs_scale=scales[:],
+                        start=(c == 0),
+                        stop=(c == PASSES - 1),
+                    )
 
         def shift_out_of_psum(n, m, first, last, copy):
             for b in range(BATCH):
@@ -255,11 +224,11 @@ def tile_relativemultiheadattention_pa_k_kernel(tc, pos_embed, W_r, b_r, grad_ou
                 if lo < hi:
                     copy(
                         out=g_t[m][:, lo + 2 - b : hi + 2 - b],
-                        in_=accs[n][m][:, lo - n * GROUP : hi - n * GROUP],
+                        in_=sums[n][m][:, lo - n * GROUP : hi - n * GROUP],
                     )
 
-        def transpose_back(n, m, tiles, banks, copy):
-            bank = next_bank([P, len(tiles), P], banks)
+        def transpose_back(n, m, tiles, copy):
+            bank = next_bank([P, len(tiles), P])
             for j, tile in enumerate(tiles):
                 row0 = n * GROUP + tile * P
                 nc.tensor.transpose(bank[:, j, :], g_t[m][:, row0 : row0 + P], identity[:])
@@ -271,64 +240,43 @@ def tile_relativemultiheadattention_pa_k_kernel(tc, pos_embed, W_r, b_r, grad_ou
                 in_=result[:, 0 : len(tiles), :],
             )
 
-        issue_loads(AHEAD)
-        for i in range(SORT_AHEAD):
-            sort_words(i)
-        quantised = 0
-        multiplied = 0
-        prepared = 0
-        finished = []
+        scalar_copy, vector_copy = nc.scalar.copy, nc.vector.tensor_copy
 
-        def multiply_passes(end, leave=False):
-            for n, c in complete[multiplied:end]:
-                for m in range(M_TILES):
-                    multiply_pass((n, c), m)
-                if c == PASSES - 1 and not leave:
-                    shift_out_of_psum(n, 0, 0, GROUP, nc.vector.tensor_copy)
-                    shift_out_of_psum(n, 1, 0, GROUP, nc.vector.tensor_copy)
-                    finished.extend((n, m, i) for m in range(M_TILES))
+        issue_loads(LOADS_AHEAD)
+        leaving = []
+        for i in range(len(steps)):
+            banks_free[0] = M_TILES * (HEAD_GROUPS if i < HEAD_STEPS + 2 else 1)
+            if i < PASSES:
+                regroup_weights(i)
+            if i + 1 < len(steps):
+                sort_words(i + 1)
+            left = transpose_step(i)
+            issue_loads(loads.index((load_grad, i)) + 1 + LOADS_AHEAD)
+            if i >= 1:
+                quantise_step(i - 1)
+            for words, source in left:
+                vector_copy(out=words, in_=source)
+            if i < PASSES:
+                quantise_weights(i)
+            if leaving:
+                n, m = leaving.pop(0)
+                transpose_back(n, m, list(range(TILES)), (vector_copy, scalar_copy)[m])
+            if i >= 2:
+                multiply_step(i - 2)
+                n, c = steps[i - 2]
+                if c + STEP_PASSES == PASSES:
+                    shift_out_of_psum(n, 0, 0, GROUP, scalar_copy)
+                    shift_out_of_psum(n, 1, 0, GROUP, vector_copy)
+                    leaving += [(n, m) for m in range(M_TILES)]
 
-        for i in range(len(grads)):
-            weights = i - W_WORK_LAG
-            if 0 <= weights < PASSES:
-                regroup_weights(weights)
-            if i + SORT_AHEAD < len(grads):
-                sort_words(i + SORT_AHEAD)
-            can_quantise = min(len(complete), quantised + STEP_PASSES)
-            can_multiply = multiplied
-            while can_multiply < min(quantised, multiplied + STEP_PASSES) and complete[can_multiply][1] < prepared:
-                can_multiply += 1
-            free_banks = list(range(M_TILES * (HEAD_GROUPS if multiplied < HEAD_GROUPS * PASSES else 1), 8))
-            if i < MULTIPLY_FIRST:
-                multiply_passes(can_multiply)
-                multiplied = can_multiply
-            transpose_load(i, free_banks)
-            issue_loads(loads.index((load_grad, i)) + 1 + AHEAD)
-            for key in complete[quantised:can_quantise]:
-                quantise_pass(key)
-            quantised = can_quantise
-            while for_vector:
-                words, source = for_vector.pop(0)
-                nc.vector.tensor_copy(out=words, in_=source)
-            if 0 <= weights < PASSES:
-                quantise_weights(weights)
-                prepared = weights + 1
-            if finished and finished[0][2] + RESULT_LAG <= i:
-                done, m, since = finished.pop(0)
-                transpose_back(done, m, list(range(TILES)), free_banks, (nc.scalar.copy, nc.vector.tensor_copy)[m])
-            if i >= MULTIPLY_FIRST:
-                multiply_passes(can_multiply)
-                multiplied = can_multiply
-
-        for key in complete[quantised:]:
-            quantise_pass(key)
-        multiply_passes(len(complete), leave=True)
-        last = GROUPS - 1
-        copies = (nc.scalar.copy, nc.vector.tensor_copy)
+        last_group = GROUPS - 1
+        quantise_step(len(steps) - 1)
+        multiply_step(len(steps) - 2)
+        multiply_step(len(steps) - 1)
         parts = [list(range(first, first + PAIR)) for first in range(0, TILES, PAIR)]
         for tiles in parts:
-            for m in range(M_TILES):
-                shift_out_of_psum(last, m, tiles[0] * P, (tiles[-1] + 1) * P, copies[m])
+            for m, copy in enumerate((scalar_copy, vector_copy)):
+                shift_out_of_psum(last_group, m, tiles[0] * P, (tiles[-1] + 1) * P, copy)
         for tiles in parts:
-            for m in range(M_TILES):
-                transpose_back(last, m, tiles, free_banks, copies[m])
+            for m, copy in enumerate((scalar_copy, vector_copy)):
+                transpose_back(last_group, m, tiles, copy)

@@ -23,17 +23,20 @@ GROUPS = TOKENS // GROUP
 TILES = GROUP // P
 M_TILES = D_IN // P
 PAIR = 2
+TWIN = 2
 
-STEP_PASSES = 2
-STEP_K = STEP_PASSES * K_PASS
-ROWS = TILES * STEP_PASSES
+UNIT_ROWS = 8
+BLOCK = 4
 HEAD_GROUPS = 2
-HEAD_STEPS = HEAD_GROUPS * PASSES // STEP_PASSES
+HEAD_UNITS = HEAD_GROUPS * PASSES * TILES // UNIT_ROWS
 
-PLAIN_STEPS = 4
-BUSY_STEPS = HEAD_STEPS + 3
-BUSY_ROWS = 4
+PLAIN_UNITS = 4
+BUSY_UNITS = HEAD_UNITS + 1
+BUSY_ROWS = (6, 4)
 FREE_ROWS = 8
+
+SCALAR_COLUMNS = 128
+SCALAR_FROM = 2 * TWIN
 
 GRAD_BUFS = 9
 LOADS_AHEAD = 12
@@ -46,15 +49,16 @@ def tile_relativemultiheadattention_pa_k_kernel(tc, pos_embed, W_r, b_r, grad_ou
     nc = tc.nc
     grad_rows = grad_out.flatten_outer_dims()
     out_rows = out.flatten_outer_dims()
+    scalar_copy, vector_copy = nc.scalar.copy, nc.vector.tensor_copy
 
     with ExitStack() as ctx:
         keep = ctx.enter_context(tc.tile_pool(name="keep", bufs=1))
         grad_pool = ctx.enter_context(tc.tile_pool(name="grad", bufs=GRAD_BUFS))
         w_raw_pool = ctx.enter_context(tc.tile_pool(name="w_raw", bufs=4))
-        w_grouped_pool = ctx.enter_context(tc.tile_pool(name="w_grouped", bufs=3))
-        sorted_pool = ctx.enter_context(tc.tile_pool(name="sorted", bufs=3))
-        grouped_pool = ctx.enter_context(tc.tile_pool(name="grouped", bufs=9))
-        operand_pool = ctx.enter_context(tc.tile_pool(name="operand", bufs=10))
+        w_grouped_pool = ctx.enter_context(tc.tile_pool(name="w_grouped", bufs=2))
+        sorted_pool = ctx.enter_context(tc.tile_pool(name="sorted", bufs=2))
+        grouped_pool = ctx.enter_context(tc.tile_pool(name="grouped", bufs=5))
+        operand_pool = ctx.enter_context(tc.tile_pool(name="operand", bufs=5))
         result_pool = ctx.enter_context(tc.tile_pool(name="result", bufs=4))
         psum = ctx.enter_context(tc.psum_pool(name="psum", bufs=1))
         ctx.enter_context(tc.manual_schedule())
@@ -69,40 +73,47 @@ def tile_relativemultiheadattention_pa_k_kernel(tc, pos_embed, W_r, b_r, grad_ou
         for m in range(M_TILES):
             nc.vector.memset(g_t[m][:, 0:8], 0.0)
 
-        steps = [(n, c) for c in range(0, PASSES, STEP_PASSES) for n in range(HEAD_GROUPS)]
-        steps += [(n, c) for n in range(HEAD_GROUPS, GROUPS) for c in range(0, PASSES, STEP_PASSES)]
+        def long_units(n, first_pass):
+            return [(n, tile, PAIR, first_pass, BLOCK) for tile in range(0, TILES, PAIR)]
+
+        def wide_units(n, first_pass):
+            return [(n, 0, TILES, c, TWIN) for c in range(first_pass, first_pass + BLOCK, TWIN)]
+
+        blocks = [(n, c) for c in range(0, PASSES, BLOCK) for n in range(HEAD_GROUPS)]
+        blocks += [(n, c) for n in range(HEAD_GROUPS, GROUPS) for c in range(0, PASSES, BLOCK)]
+        units = []
+        for n, c in blocks:
+            units += (wide_units if (n, c) == blocks[-1] else long_units)(n, c)
 
         raws, w_raws = {}, {}
 
         def load_grad(i):
-            n, c = steps[i]
-            raw = grad_pool.tile([P, TILES, STEP_PASSES, K_PASS], BF16, name="grad_raw")
-            size = PAIR if i == 0 else TILES
-            for first in range(0, TILES, size):
-                row0 = n * GROUP + first * P
-                rows = grad_rows[row0 : row0 + size * P, c * K_PASS : c * K_PASS + STEP_K]
-                nc.sync.dma_start(
-                    out=raw[:, first : first + size, :, :].rearrange("p s g k -> p s (g k)"),
-                    in_=rows.rearrange("(s p) k -> p s k", p=P),
-                )
+            n, tile, tiles, c, passes = units[i]
+            raw = grad_pool.tile([P, tiles, passes, K_PASS], BF16, name="grad_raw")
+            row0 = n * GROUP + tile * P
+            rows = grad_rows[row0 : row0 + tiles * P, c * K_PASS : (c + passes) * K_PASS]
+            nc.sync.dma_start(
+                out=raw[:].rearrange("p s g k -> p s (g k)"),
+                in_=rows.rearrange("(s p) k -> p s k", p=P),
+            )
             raws[i] = raw
 
         def load_weights(c):
-            w_raw = w_raw_pool.tile([P, STEP_PASSES, PACK, D_IN], BF16, name="w_raw")
-            rows = W_r[c * K_PASS : c * K_PASS + STEP_K, :]
+            w_raw = w_raw_pool.tile([P, TWIN, PACK, D_IN], BF16, name="w_raw")
+            rows = W_r[c * K_PASS : (c + TWIN) * K_PASS, :]
             nc.sync.dma_start(
                 out=w_raw[:].rearrange("p g t d -> p g (t d)"),
                 in_=rows.rearrange("(g p t) d -> p g (t d)", p=P, t=PACK),
             )
-            for g in range(STEP_PASSES):
-                w_raws[c + g] = w_raw[:, g, :, :]
+            w_raws[c] = w_raw
+
+        weights_at = {c: c for c in range(0, PASSES, TWIN)}
 
         loads = []
-        for i in range(len(steps)):
-            n, c = steps[i]
+        for i in range(len(units)):
             loads.append((load_grad, i))
-            if n == 0:
-                loads.append((load_weights, c))
+            if i in weights_at:
+                loads.append((load_weights, weights_at[i]))
         issued = [0]
 
         def issue_loads(count):
@@ -113,33 +124,39 @@ def tile_relativemultiheadattention_pa_k_kernel(tc, pos_embed, W_r, b_r, grad_ou
 
         w_grouped = {}
 
-        def regroup_weights(c):
-            tile = w_grouped_pool.tile([P, D_IN, PACK], BF16, name="w_grouped", align_bytes=64)
-            nc.vector.tensor_copy(
-                out=tile[:].rearrange("p (c i) t -> p c t i", i=4),
-                in_=w_raws[c].rearrange("p t (c i) -> p c t i", i=4),
+        def regroup_columns(c, g, columns, copy):
+            copy(
+                out=w_grouped[c][:, g, columns, :].rearrange("p (c i) t -> p c t i", i=4),
+                in_=w_raws[c][:, g, :, columns].rearrange("p t (c i) -> p c t i", i=4),
             )
-            w_grouped[c] = tile
+
+        def regroup_weights(c):
+            w_grouped[c] = w_grouped_pool.tile([P, TWIN, D_IN, PACK], BF16, name="w_grouped", align_bytes=64)
+            shared = D_IN - SCALAR_COLUMNS if c >= SCALAR_FROM else D_IN
+            regroup_columns(c, 0, slice(0, D_IN), vector_copy)
+            regroup_columns(c, 1, slice(0, shared), vector_copy)
+            if shared < D_IN:
+                regroup_columns(c, 1, slice(shared, D_IN), scalar_copy)
 
         def quantise_weights(c):
             nc.vector.quantize_mx(
-                out=w_codes[:, c, :].bitcast(E4M3X4),
-                scales=w_scales[:, c, :],
-                in_=w_grouped.pop(c)[:].rearrange("p d t -> p (d t)"),
+                out=w_codes[:, c : c + TWIN, :].rearrange("p g d -> p (g d)").bitcast(E4M3X4),
+                scales=w_scales[:, c : c + TWIN, :].rearrange("p g d -> p (g d)"),
+                in_=w_grouped.pop(c)[:].rearrange("p g d t -> p (g d t)"),
             )
 
         sorted_words = {}
 
         def sorted_rows(i):
-            if i < PLAIN_STEPS:
+            if i < PLAIN_UNITS:
                 return 0
-            return BUSY_ROWS if i < BUSY_STEPS else FREE_ROWS
+            return BUSY_ROWS[i % 2] if i < BUSY_UNITS else FREE_ROWS
 
         def sort_words(i):
             count = sorted_rows(i)
             if count > 0:
                 rows = raws[i][:].rearrange("p s g k -> p (s g) k").bitcast(F32)
-                tile = sorted_pool.tile([P, ROWS, 2, P], F32, name="sorted_words")
+                tile = sorted_pool.tile([P, UNIT_ROWS, 2, P], F32, name="sorted_words")
                 nc.vector.tensor_copy(
                     out=tile[:, 0:count, :, :],
                     in_=rows[:, 0:count, :].rearrange("p x (j u) -> p x u j", u=2),
@@ -147,12 +164,15 @@ def tile_relativemultiheadattention_pa_k_kernel(tc, pos_embed, W_r, b_r, grad_ou
                 sorted_words[i] = tile
 
         def words_of(i, tile, g, u):
-            row = tile * STEP_PASSES + g
+            passes = units[i][4]
+            row = tile * passes + g
             if row < sorted_rows(i):
                 return sorted_words[i][:, row, u, :]
             return raws[i][:, tile, g, :].bitcast(F32)[:, u:WORDS:2]
 
         grouped, operands, sums = {}, {}, {}
+        tiles_done = {}
+        complete = []
         banks_free = [0]
         bank_turn = [0]
 
@@ -161,61 +181,67 @@ def tile_relativemultiheadattention_pa_k_kernel(tc, pos_embed, W_r, b_r, grad_ou
             bank_turn[0] += 1
             return psum.tile(shape, F32, name="bank%d" % (banks_free[0] + bank_turn[0] % count))
 
-        def transpose_step(i):
-            left = []
-            for g in range(STEP_PASSES):
-                tile = grouped_pool.tile([P, GROUP, PACK], BF16, name="grouped", align_bytes=64)
-                grouped[(i, g)] = tile
-                for first in range(0, TILES, PAIR):
+        def transpose_unit(i):
+            n, first_tile, tiles, first_pass, passes = units[i]
+            for g in range(passes):
+                c = first_pass + g
+                twin = (n, c - c % TWIN)
+                if twin not in grouped:
+                    grouped[twin] = grouped_pool.tile([P, TWIN, GROUP, PACK], BF16, name="grouped", align_bytes=64)
+                for first in range(0, tiles, PAIR):
                     bank = next_bank([P, 2, PAIR * P])
                     for j in range(PAIR):
                         for u in range(2):
                             nc.tensor.transpose(
                                 bank[:, u, j * P : (j + 1) * P], words_of(i, first + j, g, u), identity[:]
                             )
+                    token0 = (first_tile + first) * P
                     words = (
-                        tile[:, first * P : (first + PAIR) * P, :]
+                        grouped[twin][:, c % TWIN, token0 : token0 + PAIR * P, :]
                         .rearrange("p r t -> p (r t)")
                         .bitcast(F32)
                         .rearrange("p (r u) -> p r u", u=2)
                     )
-                    source = bank[:].rearrange("p u r -> p r u")
-                    if i == len(steps) - 1 and (g, first) == (1, PAIR):
-                        left.append((words, source))
-                    else:
-                        nc.scalar.copy(out=words, in_=source)
-            return left
+                    nc.scalar.copy(out=words, in_=bank[:].rearrange("p u r -> p r u"))
+                tiles_done[twin] = tiles_done.get(twin, 0) + tiles
+                if tiles_done[twin] == TWIN * TILES:
+                    complete.append(twin)
 
-        def quantise_step(i):
-            for g in range(STEP_PASSES):
-                codes = operand_pool.tile([P, GROUP], U32, name="grad_codes", align_bytes=64)
-                scales = operand_pool.tile([P, GROUP], U8, name="grad_scales", align_bytes=64)
+        def quantise_twin(twin, at_a_time=TWIN):
+            codes = operand_pool.tile([P, TWIN, GROUP], U32, name="grad_codes", align_bytes=64)
+            scales = operand_pool.tile([P, TWIN, GROUP], U8, name="grad_scales", align_bytes=64)
+            tile = grouped.pop(twin)
+            for g in range(0, TWIN, at_a_time):
+                passes = slice(g, g + at_a_time)
                 nc.vector.quantize_mx(
-                    out=codes[:].bitcast(E5M2X4),
-                    scales=scales[:],
-                    in_=grouped.pop((i, g))[:].rearrange("p r t -> p (r t)"),
+                    out=codes[:, passes, :].rearrange("p g r -> p (g r)").bitcast(E5M2X4),
+                    scales=scales[:, passes, :].rearrange("p g r -> p (g r)"),
+                    in_=tile[:, passes, :, :].rearrange("p g r t -> p (g r t)"),
                 )
-                operands[(i, g)] = codes, scales
+            operands[twin] = codes, scales
 
-        def multiply_step(i):
-            n, first_pass = steps[i]
-            if first_pass == 0:
+        def multiply_pass(twin, g, m):
+            n, first_pass = twin
+            if n not in sums:
                 first_bank = M_TILES * (n % HEAD_GROUPS)
-                sums[n] = [psum.tile([P, GROUP], F32, name="bank%d" % (first_bank + m)) for m in range(M_TILES)]
-            for g in range(STEP_PASSES):
-                codes, scales = operands.pop((i, g))
-                c = first_pass + g
+                sums[n] = [psum.tile([P, GROUP], F32, name="bank%d" % (first_bank + j)) for j in range(M_TILES)]
+            codes, scales = operands[twin]
+            c = first_pass + g
+            columns = slice(m * P, (m + 1) * P)
+            nc.tensor.matmul_mx(
+                out=sums[n][m][:],
+                lhsT=w_codes[:, c, columns].bitcast(E4M3X4),
+                lhsT_scale=w_scales[:, c, columns],
+                rhs=codes[:, g, :].bitcast(E5M2X4),
+                rhs_scale=scales[:, g, :],
+                start=(c == 0),
+                stop=(c == PASSES - 1),
+            )
+
+        def multiply_twin(twin):
+            for g in range(TWIN):
                 for m in range(M_TILES):
-                    columns = slice(m * P, (m + 1) * P)
-                    nc.tensor.matmul_mx(
-                        out=sums[n][m][:],
-                        lhsT=w_codes[:, c, columns].bitcast(E4M3X4),
-                        lhsT_scale=w_scales[:, c, columns],
-                        rhs=codes[:].bitcast(E5M2X4),
-                        rhs_scale=scales[:],
-                        start=(c == 0),
-                        stop=(c == PASSES - 1),
-                    )
+                    multiply_pass(twin, g, m)
 
         def shift_out_of_psum(n, m, first, last, copy):
             for b in range(BATCH):
@@ -240,43 +266,51 @@ def tile_relativemultiheadattention_pa_k_kernel(tc, pos_embed, W_r, b_r, grad_ou
                 in_=result[:, 0 : len(tiles), :],
             )
 
-        scalar_copy, vector_copy = nc.scalar.copy, nc.vector.tensor_copy
-
         issue_loads(LOADS_AHEAD)
         leaving = []
-        for i in range(len(steps)):
-            banks_free[0] = M_TILES * (HEAD_GROUPS if i < HEAD_STEPS + 2 else 1)
-            if i < PASSES:
-                regroup_weights(i)
-            if i + 1 < len(steps):
+        quantised = multiplied = 0
+        groups_left = 0
+        for i in range(len(units)):
+            banks_free[0] = M_TILES * (HEAD_GROUPS if groups_left < HEAD_GROUPS else 1)
+            if i - 1 in weights_at and i > 1:
+                quantise_weights(weights_at[i - 1])
+            if quantised < len(complete):
+                quantise_twin(complete[quantised])
+                quantised += 1
+            if i in weights_at:
+                regroup_weights(weights_at[i])
+                if i == 0:
+                    quantise_weights(0)
+            if i + 1 < len(units):
                 sort_words(i + 1)
-            left = transpose_step(i)
+            transpose_unit(i)
             issue_loads(loads.index((load_grad, i)) + 1 + LOADS_AHEAD)
-            if i >= 1:
-                quantise_step(i - 1)
-            for words, source in left:
-                vector_copy(out=words, in_=source)
-            if i < PASSES:
-                quantise_weights(i)
             if leaving:
                 n, m = leaving.pop(0)
-                transpose_back(n, m, list(range(TILES)), (vector_copy, scalar_copy)[m])
-            if i >= 2:
-                multiply_step(i - 2)
-                n, c = steps[i - 2]
-                if c + STEP_PASSES == PASSES:
-                    shift_out_of_psum(n, 0, 0, GROUP, scalar_copy)
-                    shift_out_of_psum(n, 1, 0, GROUP, vector_copy)
+                transpose_back(n, m, list(range(TILES)), (scalar_copy, vector_copy)[m])
+            if multiplied < quantised:
+                n, c = complete[multiplied]
+                multiply_twin((n, c))
+                multiplied += 1
+                if c + TWIN == PASSES:
+                    groups_left += 1
+                    shift_out_of_psum(n, 0, 0, GROUP, vector_copy)
+                    shift_out_of_psum(n, 1, 0, GROUP, scalar_copy)
                     leaving += [(n, m) for m in range(M_TILES)]
 
         last_group = GROUPS - 1
-        quantise_step(len(steps) - 1)
-        multiply_step(len(steps) - 2)
-        multiply_step(len(steps) - 1)
-        parts = [list(range(first, first + PAIR)) for first in range(0, TILES, PAIR)]
-        for tiles in parts:
-            for m, copy in enumerate((scalar_copy, vector_copy)):
+        rest = complete[multiplied:]
+        for twin in complete[quantised:]:
+            quantise_twin(twin, at_a_time=1 if twin == rest[-1] else TWIN)
+        for twin in rest[:-1]:
+            multiply_twin(twin)
+        for m in range(M_TILES):
+            for g in range(TWIN):
+                multiply_pass(rest[-1], g, m)
+        halves = [list(range(first, first + PAIR)) for first in range(0, TILES, PAIR)]
+        for m in range(M_TILES):
+            for tiles, copy in zip(halves, (scalar_copy, vector_copy)):
                 shift_out_of_psum(last_group, m, tiles[0] * P, (tiles[-1] + 1) * P, copy)
-        for tiles in parts:
-            for m, copy in enumerate((scalar_copy, vector_copy)):
+        for m in range(M_TILES):
+            for tiles, copy in zip(halves, (scalar_copy, vector_copy)):
                 transpose_back(last_group, m, tiles, copy)

@@ -32,13 +32,13 @@ HEAD_UNITS = HEAD_GROUPS * PASSES * TILES // UNIT_ROWS
 
 PLAIN_UNITS = 4
 BUSY_UNITS = HEAD_UNITS + 1
-BUSY_ROWS = (6, 4)
+BUSY_ROWS = (8, 4)
 FREE_ROWS = 8
 
 SCALAR_COLUMNS = 128
 SCALAR_FROM = 2 * TWIN
 
-GRAD_BUFS = 9
+GRAD_BUFS = 7
 LOADS_AHEAD = 12
 
 FLOPS = 2 * TOKENS * D_OUT * D_IN
@@ -159,15 +159,16 @@ def tile_relativemultiheadattention_pa_k_kernel(tc, pos_embed, W_r, b_r, grad_ou
                 tile = sorted_pool.tile([P, UNIT_ROWS, 2, P], F32, name="sorted_words")
                 nc.vector.tensor_copy(
                     out=tile[:, 0:count, :, :],
-                    in_=rows[:, 0:count, :].rearrange("p x (j u) -> p x u j", u=2),
+                    in_=rows[:, UNIT_ROWS - count :, :].rearrange("p x (j u) -> p x u j", u=2),
                 )
                 sorted_words[i] = tile
 
         def words_of(i, tile, g, u):
             passes = units[i][4]
             row = tile * passes + g
-            if row < sorted_rows(i):
-                return sorted_words[i][:, row, u, :]
+            first_sorted = UNIT_ROWS - sorted_rows(i)
+            if row >= first_sorted:
+                return sorted_words[i][:, row - first_sorted, u, :]
             return raws[i][:, tile, g, :].bitcast(F32)[:, u:WORDS:2]
 
         grouped, operands, sums = {}, {}, {}

from contextlib import ExitStack

import concourse.mybir as mybir
from concourse.masks import make_identity

F32 = mybir.dt.float32
BF16 = mybir.dt.bfloat16
U32 = mybir.dt.uint32
U8 = mybir.dt.uint8
E4M3X4 = mybir.dt.float8_e4m3fn_x4
E5M2X4 = mybir.dt.float8_e5m2_x4

BATCH, SEQ, D_IN, D_OUT = 3, 512, 256, 8192
TOKENS = BATCH * SEQ

P = 128
PACK = 4
K_PASS = P * PACK
WORDS = K_PASS // 2
PASSES = D_OUT // K_PASS
GROUP = 512
GROUPS = TOKENS // GROUP
TILES = GROUP // P
M_TILES = D_IN // P
PAIR = 2
TWIN = 2

UNIT_ROWS = 8
BLOCK = 4
HEAD_GROUPS = 2
HEAD_UNITS = HEAD_GROUPS * PASSES * TILES // UNIT_ROWS

PLAIN_UNITS = 4
BUSY_UNITS = HEAD_UNITS + 1
BUSY_ROWS = (8, 4)
FREE_ROWS = 8

SCALAR_COLUMNS = 128
SCALAR_FROM = 2 * TWIN

GRAD_BUFS = 7
LOADS_AHEAD = 12

FLOPS = 2 * TOKENS * D_OUT * D_IN
BYTES = 2 * TOKENS * D_OUT + 2 * D_OUT * D_IN + 4 * TOKENS * D_IN


def tile_relativemultiheadattention_pa_k_kernel(tc, pos_embed, W_r, b_r, grad_out, out):
    nc = tc.nc
    grad_rows = grad_out.flatten_outer_dims()
    out_rows = out.flatten_outer_dims()
    scalar_copy, vector_copy = nc.scalar.copy, nc.vector.tensor_copy

    with ExitStack() as ctx:
        keep = ctx.enter_context(tc.tile_pool(name="keep", bufs=1))
        grad_pool = ctx.enter_context(tc.tile_pool(name="grad", bufs=GRAD_BUFS))
        w_raw_pool = ctx.enter_context(tc.tile_pool(name="w_raw", bufs=4))
        w_grouped_pool = ctx.enter_context(tc.tile_pool(name="w_grouped", bufs=2))
        sorted_pool = ctx.enter_context(tc.tile_pool(name="sorted", bufs=2))
        grouped_pool = ctx.enter_context(tc.tile_pool(name="grouped", bufs=5))
        operand_pool = ctx.enter_context(tc.tile_pool(name="operand", bufs=5))
        result_pool = ctx.enter_context(tc.tile_pool(name="result", bufs=4))
        psum = ctx.enter_context(tc.psum_pool(name="psum", bufs=1))
        ctx.enter_context(tc.manual_schedule())

        identity = keep.tile([P, P], F32, name="identity")
        make_identity(nc, identity[:])

        w_codes = keep.tile([P, PASSES, D_IN], U32, name="w_codes", align_bytes=64)
        w_scales = keep.tile([P, PASSES, D_IN], U8, name="w_scales", align_bytes=64)

        g_t = [keep.tile([P, TOKENS], F32, name="g_t%d" % m) for m in range(M_TILES)]
        for m in range(M_TILES):
            nc.vector.memset(g_t[m][:, 0:8], 0.0)

        def long_units(n, first_pass):
            return [(n, tile, PAIR, first_pass, BLOCK) for tile in range(0, TILES, PAIR)]

        def wide_units(n, first_pass):
            return [(n, 0, TILES, c, TWIN) for c in range(first_pass, first_pass + BLOCK, TWIN)]

        blocks = [(n, c) for c in range(0, PASSES, BLOCK) for n in range(HEAD_GROUPS)]
        blocks += [(n, c) for n in range(HEAD_GROUPS, GROUPS) for c in range(0, PASSES, BLOCK)]
        units = []
        for n, c in blocks:
            units += (wide_units if (n, c) == blocks[-1] else long_units)(n, c)

        raws, w_raws = {}, {}

        def load_grad(i):
            n, tile, tiles, c, passes = units[i]
            raw = grad_pool.tile([P, tiles, passes, K_PASS], BF16, name="grad_raw")
            row0 = n * GROUP + tile * P
            rows = grad_rows[row0 : row0 + tiles * P, c * K_PASS : (c + passes) * K_PASS]
            nc.sync.dma_start(
                out=raw[:].rearrange("p s g k -> p s (g k)"),
                in_=rows.rearrange("(s p) k -> p s k", p=P),
            )
            raws[i] = raw

        def load_weights(c):
            w_raw = w_raw_pool.tile([P, TWIN, PACK, D_IN], BF16, name="w_raw")
            rows = W_r[c * K_PASS : (c + TWIN) * K_PASS, :]
            nc.sync.dma_start(
                out=w_raw[:].rearrange("p g t d -> p g (t d)"),
                in_=rows.rearrange("(g p t) d -> p g (t d)", p=P, t=PACK),
            )
            w_raws[c] = w_raw

        weights_at = {c: c for c in range(0, PASSES, TWIN)}

        loads = []
        for i in range(len(units)):
            loads.append((load_grad, i))
            if i in weights_at:
                loads.append((load_weights, weights_at[i]))
        issued = [0]

        def issue_loads(count):
            while issued[0] < min(count, len(loads)):
                load, argument = loads[issued[0]]
                issued[0] += 1
                load(argument)

        w_grouped = {}

        def regroup_columns(c, g, columns, copy):
            copy(
                out=w_grouped[c][:, g, columns, :].rearrange("p (c i) t -> p c t i", i=4),
                in_=w_raws[c][:, g, :, columns].rearrange("p t (c i) -> p c t i", i=4),
            )

        def regroup_weights(c):
            w_grouped[c] = w_grouped_pool.tile([P, TWIN, D_IN, PACK], BF16, name="w_grouped", align_bytes=64)
            shared = D_IN - SCALAR_COLUMNS if c >= SCALAR_FROM else D_IN
            regroup_columns(c, 0, slice(0, D_IN), vector_copy)
            regroup_columns(c, 1, slice(0, shared), vector_copy)
            if shared < D_IN:
                regroup_columns(c, 1, slice(shared, D_IN), scalar_copy)

        def quantise_weights(c):
            nc.vector.quantize_mx(
                out=w_codes[:, c : c + TWIN, :].rearrange("p g d -> p (g d)").bitcast(E4M3X4),
                scales=w_scales[:, c : c + TWIN, :].rearrange("p g d -> p (g d)"),
                in_=w_grouped.pop(c)[:].rearrange("p g d t -> p (g d t)"),
            )

        sorted_words = {}

        def sorted_rows(i):
            if i < PLAIN_UNITS:
                return 0
            return BUSY_ROWS[i % 2] if i < BUSY_UNITS else FREE_ROWS

        def sort_words(i):
            count = sorted_rows(i)
            if count > 0:
                rows = raws[i][:].rearrange("p s g k -> p (s g) k").bitcast(F32)
                tile = sorted_pool.tile([P, UNIT_ROWS, 2, P], F32, name="sorted_words")
                nc.vector.tensor_copy(
                    out=tile[:, 0:count, :, :],
                    in_=rows[:, UNIT_ROWS - count :, :].rearrange("p x (j u) -> p x u j", u=2),
                )
                sorted_words[i] = tile

        def words_of(i, tile, g, u):
            passes = units[i][4]
            row = tile * passes + g
            first_sorted = UNIT_ROWS - sorted_rows(i)
            if row >= first_sorted:
                return sorted_words[i][:, row - first_sorted, u, :]
            return raws[i][:, tile, g, :].bitcast(F32)[:, u:WORDS:2]

        grouped, operands, sums = {}, {}, {}
        tiles_done = {}
        complete = []
        banks_free = [0]
        bank_turn = [0]

        def next_bank(shape):
            count = 8 - banks_free[0]
            bank_turn[0] += 1
            return psum.tile(shape, F32, name="bank%d" % (banks_free[0] + bank_turn[0] % count))

        def transpose_unit(i):
            n, first_tile, tiles, first_pass, passes = units[i]
            for g in range(passes):
                c = first_pass + g
                twin = (n, c - c % TWIN)
                if twin not in grouped:
                    grouped[twin] = grouped_pool.tile([P, TWIN, GROUP, PACK], BF16, name="grouped", align_bytes=64)
                for first in range(0, tiles, PAIR):
                    bank = next_bank([P, 2, PAIR * P])
                    for j in range(PAIR):
                        for u in range(2):
                            nc.tensor.transpose(
                                bank[:, u, j * P : (j + 1) * P], words_of(i, first + j, g, u), identity[:]
                            )
                    token0 = (first_tile + first) * P
                    words = (
                        grouped[twin][:, c % TWIN, token0 : token0 + PAIR * P, :]
                        .rearrange("p r t -> p (r t)")
                        .bitcast(F32)
                        .rearrange("p (r u) -> p r u", u=2)
                    )
                    nc.scalar.copy(out=words, in_=bank[:].rearrange("p u r -> p r u"))
                tiles_done[twin] = tiles_done.get(twin, 0) + tiles
                if tiles_done[twin] == TWIN * TILES:
                    complete.append(twin)

        def quantise_twin(twin, at_a_time=TWIN):
            codes = operand_pool.tile([P, TWIN, GROUP], U32, name="grad_codes", align_bytes=64)
            scales = operand_pool.tile([P, TWIN, GROUP], U8, name="grad_scales", align_bytes=64)
            tile = grouped.pop(twin)
            for g in range(0, TWIN, at_a_time):
                passes = slice(g, g + at_a_time)
                nc.vector.quantize_mx(
                    out=codes[:, passes, :].rearrange("p g r -> p (g r)").bitcast(E5M2X4),
                    scales=scales[:, passes, :].rearrange("p g r -> p (g r)"),
                    in_=tile[:, passes, :, :].rearrange("p g r t -> p (g r t)"),
                )
            operands[twin] = codes, scales

        def multiply_pass(twin, g, m):
            n, first_pass = twin
            if n not in sums:
                first_bank = M_TILES * (n % HEAD_GROUPS)
                sums[n] = [psum.tile([P, GROUP], F32, name="bank%d" % (first_bank + j)) for j in range(M_TILES)]
            codes, scales = operands[twin]
            c = first_pass + g
            columns = slice(m * P, (m + 1) * P)
            nc.tensor.matmul_mx(
                out=sums[n][m][:],
                lhsT=w_codes[:, c, columns].bitcast(E4M3X4),
                lhsT_scale=w_scales[:, c, columns],
                rhs=codes[:, g, :].bitcast(E5M2X4),
                rhs_scale=scales[:, g, :],
                start=(c == 0),
                stop=(c == PASSES - 1),
            )

        def multiply_twin(twin):
            for g in range(TWIN):
                for m in range(M_TILES):
                    multiply_pass(twin, g, m)

        def shift_out_of_psum(n, m, first, last, copy):
            for b in range(BATCH):
                lo = max((SEQ + 1) * b - 2, n * GROUP + first)
                hi = min((SEQ + 1) * b - 2 + SEQ, n * GROUP + last)
                if lo < hi:
                    copy(
                        out=g_t[m][:, lo + 2 - b : hi + 2 - b],
                        in_=sums[n][m][:, lo - n * GROUP : hi - n * GROUP],
                    )

        def transpose_back(n, m, tiles, copy):
            bank = next_bank([P, len(tiles), P])
            for j, tile in enumerate(tiles):
                row0 = n * GROUP + tile * P
                nc.tensor.transpose(bank[:, j, :], g_t[m][:, row0 : row0 + P], identity[:])
            result = result_pool.tile([P, TILES, P], F32, name="result")
            copy(out=result[:, 0 : len(tiles), :], in_=bank[:])
            row0 = n * GROUP + tiles[0] * P
            nc.sync.dma_start(
                out=out_rows[row0 : row0 + len(tiles) * P, m * P : (m + 1) * P].rearrange("(j p) d -> p j d", p=P),
                in_=result[:, 0 : len(tiles), :],
            )

        issue_loads(LOADS_AHEAD)
        leaving = []
        quantised = multiplied = 0
        groups_left = 0
        for i in range(len(units)):
            banks_free[0] = M_TILES * (HEAD_GROUPS if groups_left < HEAD_GROUPS else 1)
            if i - 1 in weights_at and i > 1:
                quantise_weights(weights_at[i - 1])
            if quantised < len(complete):
                quantise_twin(complete[quantised])
                quantised += 1
            if i in weights_at:
                regroup_weights(weights_at[i])
                if i == 0:
                    quantise_weights(0)
            if i + 1 < len(units):
                sort_words(i + 1)
            transpose_unit(i)
            issue_loads(loads.index((load_grad, i)) + 1 + LOADS_AHEAD)
            if leaving:
                n, m = leaving.pop(0)
                transpose_back(n, m, list(range(TILES)), (scalar_copy, vector_copy)[m])
            if multiplied < quantised:
                n, c = complete[multiplied]
                multiply_twin((n, c))
                multiplied += 1
                if c + TWIN == PASSES:
                    groups_left += 1
                    shift_out_of_psum(n, 0, 0, GROUP, vector_copy)
                    shift_out_of_psum(n, 1, 0, GROUP, scalar_copy)
                    leaving += [(n, m) for m in range(M_TILES)]

        last_group = GROUPS - 1
        rest = complete[multiplied:]
        for twin in complete[quantised:]:
            quantise_twin(twin, at_a_time=1 if twin == rest[-1] else TWIN)
        for twin in rest[:-1]:
            multiply_twin(twin)
        for m in range(M_TILES):
            for g in range(TWIN):
                multiply_pass(rest[-1], g, m)
        halves = [list(range(first, first + PAIR)) for first in range(0, TILES, PAIR)]
        for m in range(M_TILES):
            for tiles, copy in zip(halves, (scalar_copy, vector_copy)):
                shift_out_of_psum(last_group, m, tiles[0] * P, (tiles[-1] + 1) * P, copy)
        for m in range(M_TILES):
            for tiles, copy in zip(halves, (scalar_copy, vector_copy)):
                transpose_back(last_group, m, tiles, copy)
